import numpy as np
import ml_dtypes


def mxq(x, axis, fmt="e4m3"):
    dtype, down = {"e4m3": (ml_dtypes.float8_e4m3fn, 7), "e5m2": (ml_dtypes.float8_e5m2, 14)}[fmt]
    v = np.moveaxis(np.asarray(x, np.float32).astype(ml_dtypes.bfloat16).astype(np.float64), axis, -1)
    blocks = v.reshape(v.shape[:-1] + (-1, 32))
    amax = np.abs(blocks).max(-1, keepdims=True)
    byte = np.maximum(np.where(amax > 0, np.frexp(amax)[1] - 1 + 127, 0) - down, 1)
    scale = np.exp2(byte - 127.0)
    codes = (blocks / scale).astype(np.float32).astype(dtype).astype(np.float64)
    return np.moveaxis((codes * scale).reshape(v.shape), -1, axis)


WIDE = False


def mx_kscale(k):
    if not WIDE:
        return np.ones(k)
    levels = np.array([20, -20, 10, -10, 0])
    a = np.random.permutation(np.resize(levels, k // 512 * 4)).reshape(k // 512, 4)
    idx = np.arange(k)
    return np.exp2(a[idx // 512, idx % 128 // 32])


BF16 = ml_dtypes.bfloat16


def bf(x):
    return np.asarray(x, np.float32).astype(BF16)


def f64(x):
    return np.asarray(x).astype(np.float64)


B, NH, NW, C, K, P = 8, 32, 32, 64, 64, 4
T = P * P
N = B * NH * NW
HAD = np.array([[1.0, 1.0, 1.0, 1.0],
                [1.0, -1.0, 1.0, -1.0],
                [1.0, 1.0, -1.0, -1.0],
                [1.0, -1.0, -1.0, 1.0]])


def setup_inputs():
    s = mx_kscale(N).reshape(B, NH, NW)
    trans = np.random.standard_normal((T, B, NH, NW, C)) * s[None, :, :, :, None]
    weight = np.random.standard_normal((T, C, K)) * 0.5 * P / np.sqrt(C)
    bias = np.random.standard_normal((1, 1, 1, K)) * 0.2
    g = np.random.standard_normal((B, P * NH, P * NW, K))
    e = np.exp2(np.random.randint(-12, 1, (B, NH, NW))) / s
    e = np.repeat(np.repeat(e, P, axis=1), P, axis=2)[:, :, :, None]
    return {"trans": bf(trans), "weight": bf(weight), "bias": bf(bias), "grad_out": bf(g * e)}


def reference(trans, weight, bias, grad_out):
    x = f64(trans).reshape(T, N, C)
    g = f64(grad_out).reshape(B, NH, P, NW, P, K).transpose(2, 4, 0, 1, 3, 5)
    r = np.stack([sum(HAD[p, u] * g[p] for p in range(P)) for u in range(P)])
    gy = np.stack([sum(HAD[q, v] * r[:, q] for q in range(P)) for v in range(P)], axis=1) / T
    gy = gy.reshape(T, N, K)
    return mxq(x, 1, "e4m3").transpose(0, 2, 1) @ mxq(gy, 1, "e5m2")

@@ -1,0 +1,120 @@
+from contextlib import ExitStack
+
+import concourse.mybir as mybir
+
+F32 = mybir.dt.float32
+BF16 = mybir.dt.bfloat16
+U32 = mybir.dt.uint32
+U8 = mybir.dt.uint8
+E4M3_X4 = mybir.dt.float8_e4m3fn_x4
+E5M2_X4 = mybir.dt.float8_e5m2_x4
+ADD = mybir.AluOpType.add
+SUB = mybir.AluOpType.subtract
+
+PARTS = 128
+PACK = 4
+K_PASS = PARTS * PACK
+
+B, NH, NW, C, K, SIDE = 8, 32, 32, 64, 64, 4
+T = SIDE * SIDE
+N = B * NH * NW
+PASSES = N // K_PASS
+ROWS_PER_PASS = K_PASS // NW
+PARTS_PER_ROW = NW // PACK
+COLS = T * K
+ELEMS = COLS * PACK
+
+M_TILE = 128
+N_TILE = 512
+T_PER_M = M_TILE // C
+T_PER_N = N_TILE // K
+PAIRS = T // T_PER_M
+
+FLOPS = 2 * T * C * K * N + 4 * T * N * K
+BYTES = 2 * T * N * C + 2 * T * N * K + 4 * T * C * K
+
+
+def butterfly(nc, out, in_, groups, half):
+    src = in_.rearrange("p (g two e) -> p g two e", g=groups, two=2, e=half)
+    dst = out.rearrange("p (g two e) -> p g two e", g=groups, two=2, e=half)
+    nc.vector.tensor_tensor(out=dst[:, :, 0, :], in0=src[:, :, 0, :], in1=src[:, :, 1, :], op=ADD)
+    nc.vector.tensor_tensor(out=dst[:, :, 1, :], in0=src[:, :, 0, :], in1=src[:, :, 1, :], op=SUB)
+
+
+def tile_iwht3layer_pa_k_kernel(tc, trans, weight, bias, grad_out, out):
+    nc = tc.nc
+
+    x_dram = trans.rearrange(
+        "t b (h i) (r tau) c -> (b h) (i r) t (tau c)", h=2, i=ROWS_PER_PASS, r=PARTS_PER_ROW, tau=PACK
+    )
+    g_dram = grad_out.rearrange(
+        "b (h i p) (r e) k -> (b h) p i r (e k)", h=2, i=ROWS_PER_PASS, p=SIDE, r=PARTS_PER_ROW, e=PACK * SIDE
+    )
+
+    with ExitStack() as ctx:
+        raw = ctx.enter_context(tc.tile_pool(name="raw", bufs=3))
+        levels = ctx.enter_context(tc.tile_pool(name="levels", bufs=1))
+        grouped = ctx.enter_context(tc.tile_pool(name="grouped", bufs=2))
+        packed = ctx.enter_context(tc.tile_pool(name="packed", bufs=3))
+        last = ctx.enter_context(tc.tile_pool(name="last", bufs=1))
+        psum = ctx.enter_context(tc.psum_pool(name="psum", bufs=1))
+
+        acc = [psum.tile([M_TILE, N_TILE], F32, name="acc%d" % s) for s in range(PAIRS)]
+
+        for c in range(PASSES):
+            g_raw = raw.tile([PARTS, SIDE, ELEMS // SIDE], BF16)
+            for p in range(SIDE):
+                nc.sync.dma_start(out=g_raw[:, p, :], in_=g_dram[c, p])
+            x_raw = raw.tile([PARTS, T, PACK * C], BF16)
+            nc.sync.dma_start(out=x_raw[:], in_=x_dram[c])
+
+            pixels = levels.tile([PARTS, ELEMS], F32)
+            nc.scalar.activation(
+                out=pixels[:].rearrange("a (p qk tau) -> a p qk tau", p=SIDE, qk=SIDE * K, tau=PACK),
+                in_=g_raw[:].rearrange("a p (tau qk) -> a p qk tau", tau=PACK, qk=SIDE * K),
+                func=mybir.ActivationFunctionType.Copy,
+                scale=1.0 / T,
+            )
+            x_grouped = grouped.tile([PARTS, ELEMS], BF16, align_bytes=64)
+            nc.scalar.copy(
+                out=x_grouped[:].rearrange("a (t c tau) -> a t c tau", t=T, c=C, tau=PACK),
+                in_=x_raw[:].rearrange("a t (tau c) -> a t c tau", tau=PACK, c=C),
+            )
+
+            rows_hi = levels.tile([PARTS, ELEMS], F32)
+            butterfly(nc, rows_hi[:], pixels[:], 1, ELEMS // 2)
+            rows = levels.tile([PARTS, ELEMS], F32)
+            butterfly(nc, rows[:], rows_hi[:], 2, ELEMS // 4)
+            cols_hi = levels.tile([PARTS, ELEMS], F32)
+            butterfly(nc, cols_hi[:], rows[:], 4, ELEMS // 8)
+            gy_grouped = grouped.tile([PARTS, ELEMS], BF16, align_bytes=64)
+            butterfly(nc, gy_grouped[:], cols_hi[:], 8, ELEMS // 16)
+
+            x_codes = packed.tile([PARTS, COLS], U32, align_bytes=64)
+            x_scales = packed.tile([PARTS, COLS], U8, align_bytes=64)
+            nc.vector.quantize_mx(out=x_codes[:].bitcast(E4M3_X4), scales=x_scales[:], in_=x_grouped[:])
+            gy_codes = packed.tile([PARTS, COLS], U32, align_bytes=64)
+            gy_scales = packed.tile([PARTS, COLS], U8, align_bytes=64)
+            nc.vector.quantize_mx(out=gy_codes[:].bitcast(E5M2_X4), scales=gy_scales[:], in_=gy_grouped[:])
+
+            for s in range(PAIRS):
+                m_cols = slice(s * M_TILE, (s + 1) * M_TILE)
+                n_first = (s * T_PER_M // T_PER_N) * N_TILE
+                n_cols = slice(n_first, n_first + N_TILE)
+                nc.tensor.matmul_mx(
+                    out=acc[s][:],
+                    lhsT=x_codes[:, m_cols].bitcast(E4M3_X4),
+                    lhsT_scale=x_scales[:, m_cols],
+                    rhs=gy_codes[:, n_cols].bitcast(E5M2_X4),
+                    rhs_scale=gy_scales[:, n_cols],
+                    start=(c == 0),
+                    stop=(c == PASSES - 1),
+                )
+
+        result = last.tile([M_TILE, PAIRS, K], F32)
+        for s in range(PAIRS):
+            even = (s * T_PER_M % T_PER_N) * K
+            odd = even + K
+            nc.scalar.copy(out=result[0:C, s, :], in_=acc[s][0:C, even : even + K])
+            nc.vector.tensor_copy(out=result[C:M_TILE, s, :], in_=acc[s][C:M_TILE, odd : odd + K])
+        nc.sync.dma_start(out=out.rearrange("(s two) c k -> (two c) s k", two=T_PER_M), in_=result[:])

@@ -1,6 +1,7 @@
 from contextlib import ExitStack
 
 import concourse.mybir as mybir
+from concourse.masks import make_identity
 
 F32 = mybir.dt.float32
 BF16 = mybir.dt.bfloat16
@@ -10,6 +11,7 @@ E4M3_X4 = mybir.dt.float8_e4m3fn_x4
 E5M2_X4 = mybir.dt.float8_e5m2_x4
 ADD = mybir.AluOpType.add
 SUB = mybir.AluOpType.subtract
+MULT = mybir.AluOpType.mult
 
 PARTS = 128
 PACK = 4
@@ -23,22 +25,43 @@ ROWS_PER_PASS = K_PASS // NW
 PARTS_PER_ROW = NW // PACK
 COLS = T * K
 ELEMS = COLS * PACK
+LANE = K * PACK
+HALVES = LANE // PARTS
+GROUPS = SIDE * HALVES
 
 M_TILE = 128
 N_TILE = 512
 T_PER_M = M_TILE // C
 T_PER_N = N_TILE // K
 PAIRS = T // T_PER_M
+ROUND = 2
 
 FLOPS = 2 * T * C * K * N + 4 * T * N * K
 BYTES = 2 * T * N * C + 2 * T * N * K + 4 * T * C * K
 
 
-def butterfly(nc, out, in_, groups, half):
-    src = in_.rearrange("p (g two e) -> p g two e", g=groups, two=2, e=half)
-    dst = out.rearrange("p (g two e) -> p g two e", g=groups, two=2, e=half)
-    nc.vector.tensor_tensor(out=dst[:, :, 0, :], in0=src[:, :, 0, :], in1=src[:, :, 1, :], op=ADD)
-    nc.vector.tensor_tensor(out=dst[:, :, 1, :], in0=src[:, :, 0, :], in1=src[:, :, 1, :], op=SUB)
+def sums_of_two(nc, bank, four, ident):
+    for place, (first, second) in enumerate(((0, 2), (1, 3), (0, 1), (0, 3))):
+        nc.tensor.matmul(
+            out=bank[:, place, :], lhsT=four[first], rhs=ident, is_transpose=True, start=True, stop=False
+        )
+        nc.tensor.matmul(
+            out=bank[:, place, :], lhsT=four[second], rhs=ident, is_transpose=True, start=False, stop=True
+        )
+
+
+def signed_sums(nc, bank, odd, out0, out1, out23):
+    nc.scalar.copy(out=odd, in_=bank[:, 1, :])
+    nc.vector.tensor_tensor(out=out0, in0=bank[:, 0, :], in1=odd, op=ADD)
+    nc.vector.tensor_tensor(out=out1, in0=bank[:, 0, :], in1=odd, op=SUB)
+    nc.vector.scalar_tensor_tensor(
+        out=out23,
+        in0=bank[:, 2:4, :],
+        scalar=2.0,
+        in1=out0.unsqueeze(1).to_broadcast([PARTS, 2, PARTS]),
+        op0=MULT,
+        op1=SUB,
+    )
 
 
 def tile_iwht3layer_pa_k_kernel(tc, trans, weight, bias, grad_out, out):
@@ -52,69 +75,148 @@ def tile_iwht3layer_pa_k_kernel(tc, trans, weight, bias, grad_out, out):
     )
 
     with ExitStack() as ctx:
+        ctx.enter_context(tc.manual_schedule())
+        const = ctx.enter_context(tc.tile_pool(name="const", bufs=1))
         raw = ctx.enter_context(tc.tile_pool(name="raw", bufs=3))
-        levels = ctx.enter_context(tc.tile_pool(name="levels", bufs=1))
+        stages = ctx.enter_context(tc.tile_pool(name="stages", bufs=2))
+        small = ctx.enter_context(tc.tile_pool(name="small", bufs=4))
         grouped = ctx.enter_context(tc.tile_pool(name="grouped", bufs=2))
-        packed = ctx.enter_context(tc.tile_pool(name="packed", bufs=3))
-        last = ctx.enter_context(tc.tile_pool(name="last", bufs=1))
-        psum = ctx.enter_context(tc.psum_pool(name="psum", bufs=1))
+        packed = ctx.enter_context(tc.tile_pool(name="packed", bufs=4))
+        sums = ctx.enter_context(tc.psum_pool(name="sums", bufs=6))
+        products = ctx.enter_context(tc.psum_pool(name="products", bufs=2))
 
-        acc = [psum.tile([M_TILE, N_TILE], F32, name="acc%d" % s) for s in range(PAIRS)]
+        ident = const.tile([PARTS, PARTS], F32)
+        make_identity(nc, ident[:])
+        result = const.tile([M_TILE, PAIRS, M_TILE], F32)
 
-        for c in range(PASSES):
-            g_raw = raw.tile([PARTS, SIDE, ELEMS // SIDE], BF16)
+        g_raw, x_raw, pixels, rows, x_grouped, gy_grouped, codes = {}, {}, {}, {}, {}, {}, {}
+        totals = {}
+
+        def load(c):
+            g_raw[c] = raw.tile([PARTS, SIDE, SIDE * LANE], BF16, name="g_raw")
             for p in range(SIDE):
-                nc.sync.dma_start(out=g_raw[:, p, :], in_=g_dram[c, p])
-            x_raw = raw.tile([PARTS, T, PACK * C], BF16)
-            nc.sync.dma_start(out=x_raw[:], in_=x_dram[c])
+                nc.sync.dma_start(out=g_raw[c][:, p, :], in_=g_dram[c, p])
+            x_raw[c] = raw.tile([PARTS, T, LANE], BF16, name="x_raw")
+            nc.sync.dma_start(out=x_raw[c][:], in_=x_dram[c])
 
-            pixels = levels.tile([PARTS, ELEMS], F32)
+        def widen(c, piece):
+            if piece == 0:
+                pixels[c] = stages.tile([PARTS, SIDE, SIDE, LANE], F32, name="pixels")
+            q, first_p = piece // 2, 2 * (piece % 2)
             nc.scalar.activation(
-                out=pixels[:].rearrange("a (p qk tau) -> a p qk tau", p=SIDE, qk=SIDE * K, tau=PACK),
-                in_=g_raw[:].rearrange("a p (tau qk) -> a p qk tau", tau=PACK, qk=SIDE * K),
+                out=pixels[c][:, q, first_p : first_p + 2, :].rearrange("a p (k tau) -> a p k tau", tau=PACK),
+                in_=g_raw[c][:].rearrange("a p (tau q k) -> a q p k tau", tau=PACK, q=SIDE)[
+                    :, q, first_p : first_p + 2
+                ],
                 func=mybir.ActivationFunctionType.Copy,
                 scale=1.0 / T,
             )
-            x_grouped = grouped.tile([PARTS, ELEMS], BF16, align_bytes=64)
-            nc.scalar.copy(
-                out=x_grouped[:].rearrange("a (t c tau) -> a t c tau", t=T, c=C, tau=PACK),
-                in_=x_raw[:].rearrange("a t (tau c) -> a t c tau", tau=PACK, c=C),
+
+        def regroup(c, piece):
+            if piece == 0:
+                x_grouped[c] = grouped.tile([PARTS, T, LANE], BF16, name="x_grouped", align_bytes=64)
+            first_t = 2 * piece
+            nc.gpsimd.tensor_scalar(
+                out=x_grouped[c][:, first_t : first_t + 2, :].rearrange("a t (c tau) -> a t c tau", tau=PACK),
+                in0=x_raw[c][:, first_t : first_t + 2, :].rearrange("a t (tau c) -> a t c tau", tau=PACK),
+                scalar1=1.0,
+                scalar2=0.0,
+                op0=MULT,
+                op1=ADD,
             )
 
-            rows_hi = levels.tile([PARTS, ELEMS], F32)
-            butterfly(nc, rows_hi[:], pixels[:], 1, ELEMS // 2)
-            rows = levels.tile([PARTS, ELEMS], F32)
-            butterfly(nc, rows[:], rows_hi[:], 2, ELEMS // 4)
-            cols_hi = levels.tile([PARTS, ELEMS], F32)
-            butterfly(nc, cols_hi[:], rows[:], 4, ELEMS // 8)
-            gy_grouped = grouped.tile([PARTS, ELEMS], BF16, align_bytes=64)
-            butterfly(nc, gy_grouped[:], cols_hi[:], 8, ELEMS // 16)
+        def row_stage(c, group):
+            if group == 0:
+                rows[c] = stages.tile([PARTS, HALVES, SIDE, SIDE, PARTS], F32, name="rows")
+            q, half = group // HALVES, group % HALVES
+            lane = slice(half * PARTS, (half + 1) * PARTS)
+            bank = sums.tile([PARTS, SIDE, PARTS], F32, name="bank")
+            sums_of_two(nc, bank, [pixels[c][:, q, p, lane] for p in range(SIDE)], ident[:])
+            odd = small.tile([PARTS, PARTS], F32, name="odd")
+            signed_sums(
+                nc, bank, odd[:], rows[c][:, half, 0, q, :], rows[c][:, half, 1, q, :], rows[c][:, half, 2:4, q, :]
+            )
 
-            x_codes = packed.tile([PARTS, COLS], U32, align_bytes=64)
-            x_scales = packed.tile([PARTS, COLS], U8, align_bytes=64)
-            nc.vector.quantize_mx(out=x_codes[:].bitcast(E4M3_X4), scales=x_scales[:], in_=x_grouped[:])
-            gy_codes = packed.tile([PARTS, COLS], U32, align_bytes=64)
-            gy_scales = packed.tile([PARTS, COLS], U8, align_bytes=64)
-            nc.vector.quantize_mx(out=gy_codes[:].bitcast(E5M2_X4), scales=gy_scales[:], in_=gy_grouped[:])
+        def column_stage(c, group):
+            if group == 0:
+                gy_grouped[c] = grouped.tile([PARTS, T, LANE], BF16, name="gy_grouped", align_bytes=64)
+            half, u = group // SIDE, group % SIDE
+            lane = slice(half * PARTS, (half + 1) * PARTS)
+            t = SIDE * u
+            bank = sums.tile([PARTS, SIDE, PARTS], F32, name="bank")
+            sums_of_two(nc, bank, [rows[c][:, half, u, q, :] for q in range(SIDE)], ident[:])
+            odd = small.tile([PARTS, PARTS], F32, name="odd")
+            total = small.tile([PARTS, PARTS], F32, name="total")
+            signed_sums(
+                nc, bank, odd[:], total[:], gy_grouped[c][:, t + 1, lane], gy_grouped[c][:, t + 2 : t + 4, lane]
+            )
+            totals[group] = total
+            if group > 0:
+                round_total(c, group - 1)
 
+        def round_total(c, group):
+            half, u = group // SIDE, group % SIDE
+            lane = slice(half * PARTS, (half + 1) * PARTS)
+            nc.scalar.copy(out=gy_grouped[c][:, SIDE * u, lane], in_=totals[group][:])
+
+        def quantise(c):
+            round_total(c, GROUPS - 1)
+            x_codes = packed.tile([PARTS, COLS], U32, name="x_codes", align_bytes=64)
+            x_scales = packed.tile([PARTS, COLS], U8, name="x_scales", align_bytes=64)
+            nc.vector.quantize_mx(
+                out=x_codes[:].bitcast(E4M3_X4), scales=x_scales[:], in_=x_grouped[c][:].rearrange("a t e -> a (t e)")
+            )
+            gy_codes = packed.tile([PARTS, COLS], U32, name="gy_codes", align_bytes=64)
+            gy_scales = packed.tile([PARTS, COLS], U8, name="gy_scales", align_bytes=64)
+            nc.vector.quantize_mx(
+                out=gy_codes[:].bitcast(E5M2_X4), scales=gy_scales[:], in_=gy_grouped[c][:].rearrange("a t e -> a (t e)")
+            )
+            codes[c] = (x_codes, x_scales, gy_codes, gy_scales)
+
+        def multiply(first_pass):
             for s in range(PAIRS):
                 m_cols = slice(s * M_TILE, (s + 1) * M_TILE)
                 n_first = (s * T_PER_M // T_PER_N) * N_TILE
                 n_cols = slice(n_first, n_first + N_TILE)
-                nc.tensor.matmul_mx(
-                    out=acc[s][:],
-                    lhsT=x_codes[:, m_cols].bitcast(E4M3_X4),
-                    lhsT_scale=x_scales[:, m_cols],
-                    rhs=gy_codes[:, n_cols].bitcast(E5M2_X4),
-                    rhs_scale=gy_scales[:, n_cols],
-                    start=(c == 0),
-                    stop=(c == PASSES - 1),
-                )
+                product = products.tile([M_TILE, N_TILE], F32, name="product")
+                for c in range(first_pass, first_pass + ROUND):
+                    x_codes, x_scales, gy_codes, gy_scales = codes[c]
+                    nc.tensor.matmul_mx(
+                        out=product[:],
+                        lhsT=x_codes[:, m_cols].bitcast(E4M3_X4),
+                        lhsT_scale=x_scales[:, m_cols],
+                        rhs=gy_codes[:, n_cols].bitcast(E5M2_X4),
+                        rhs_scale=gy_scales[:, n_cols],
+                        start=(c == first_pass),
+                        stop=(c == first_pass + ROUND - 1),
+                    )
+                wanted = slice(s * M_TILE - n_first, (s + 1) * M_TILE - n_first)
+                if first_pass == 0:
+                    nc.vector.tensor_copy(out=result[:, s, :], in_=product[:, wanted])
+                else:
+                    nc.vector.tensor_tensor(out=result[:, s, :], in0=product[:, wanted], in1=result[:, s, :], op=ADD)
 
-        result = last.tile([M_TILE, PAIRS, K], F32)
-        for s in range(PAIRS):
-            even = (s * T_PER_M % T_PER_N) * K
-            odd = even + K
-            nc.scalar.copy(out=result[0:C, s, :], in_=acc[s][0:C, even : even + K])
-            nc.vector.tensor_copy(out=result[C:M_TILE, s, :], in_=acc[s][C:M_TILE, odd : odd + K])
-        nc.sync.dma_start(out=out.rearrange("(s two) c k -> (two c) s k", two=T_PER_M), in_=result[:])
+        load(0)
+        load(1)
+        for piece in range(GROUPS):
+            widen(0, piece)
+        for c in range(-1, PASSES):
+            if c + 3 < PASSES:
+                load(c + 3)
+            if c + 1 < PASSES:
+                for group in range(GROUPS):
+                    row_stage(c + 1, group)
+                    regroup(c + 1, group)
+                    if c + 2 < PASSES:
+                        widen(c + 2, group)
+            if c >= ROUND and c % ROUND == 0:
+                multiply(c - ROUND)
+            if c >= 0:
+                for group in range(GROUPS):
+                    column_stage(c, group)
+                quantise(c)
+        multiply(PASSES - ROUND)
+
+        out_view = out.rearrange("(s two) c k -> two c s k", two=T_PER_M)
+        nc.sync.dma_start(out=out_view[0], in_=result[0:C, :, 0:K])
+        nc.sync.dma_start(out=out_view[1], in_=result[C:M_TILE, :, K:M_TILE])

@@ -40,25 +40,28 @@ FLOPS = 2 * T * C * K * N + 4 * T * N * K
 BYTES = 2 * T * N * C + 2 * T * N * K + 4 * T * C * K
 
 
-def sums_of_two(nc, bank, four, ident):
-    for place, (first, second) in enumerate(((0, 2), (1, 3), (0, 1), (0, 3))):
-        nc.tensor.matmul(
-            out=bank[:, place, :], lhsT=four[first], rhs=ident, is_transpose=True, start=True, stop=False
-        )
-        nc.tensor.matmul(
-            out=bank[:, place, :], lhsT=four[second], rhs=ident, is_transpose=True, start=False, stop=True
-        )
+def sums_of_two(nc, bank_a, bank_b, fours, ident):
+    for bank, pairs in ((bank_a, ((0, 2), (1, 3))), (bank_b, ((0, 1), (0, 3)))):
+        for place, (first, second) in enumerate(pairs):
+            for h, four in enumerate(fours):
+                nc.tensor.matmul(
+                    out=bank[:, place, h, :], lhsT=four[first], rhs=ident, is_transpose=True, start=True, stop=False
+                )
+                nc.tensor.matmul(
+                    out=bank[:, place, h, :], lhsT=four[second], rhs=ident, is_transpose=True, start=False, stop=True
+                )
 
 
-def signed_sums(nc, bank, odd, out0, out1, out23):
-    nc.scalar.copy(out=odd, in_=bank[:, 1, :])
-    nc.vector.tensor_tensor(out=out0, in0=bank[:, 0, :], in1=odd, op=ADD)
-    nc.vector.tensor_tensor(out=out1, in0=bank[:, 0, :], in1=odd, op=SUB)
+def signed_sums(nc, bank_a, bank_b, odd, out0, out1, out23):
+    even = bank_a[:, 0, :, :].rearrange("a h e -> a (h e)")
+    nc.scalar.copy(out=odd, in_=bank_a[:, 1, :, :].rearrange("a h e -> a (h e)"))
+    nc.vector.tensor_tensor(out=out0, in0=even, in1=odd, op=ADD)
+    nc.vector.tensor_tensor(out=out1, in0=even, in1=odd, op=SUB)
     nc.vector.scalar_tensor_tensor(
         out=out23,
-        in0=bank[:, 2:4, :],
+        in0=bank_b[:].rearrange("a u h e -> a u (h e)"),
         scalar=2.0,
-        in1=out0.unsqueeze(1).to_broadcast([PARTS, 2, PARTS]),
+        in1=out0.unsqueeze(1).to_broadcast([PARTS, 2, LANE]),
         op0=MULT,
         op1=SUB,
     )
@@ -125,42 +128,40 @@ def tile_iwht3layer_pa_k_kernel(tc, trans, weight, bias, grad_out, out):
                 op1=ADD,
             )
 
-        def row_stage(c, group):
-            if group == 0:
-                rows[c] = stages.tile([PARTS, HALVES, SIDE, SIDE, PARTS], F32, name="rows")
-            q, half = group // HALVES, group % HALVES
-            lane = slice(half * PARTS, (half + 1) * PARTS)
-            bank = sums.tile([PARTS, SIDE, PARTS], F32, name="bank")
-            sums_of_two(nc, bank, [pixels[c][:, q, p, lane] for p in range(SIDE)], ident[:])
-            odd = small.tile([PARTS, PARTS], F32, name="odd")
-            signed_sums(
-                nc, bank, odd[:], rows[c][:, half, 0, q, :], rows[c][:, half, 1, q, :], rows[c][:, half, 2:4, q, :]
-            )
+        def row_stage(c, q):
+            if q == 0:
+                rows[c] = stages.tile([PARTS, SIDE, SIDE, LANE], F32, name="rows")
+            bank_a = sums.tile([PARTS, 2, HALVES, PARTS], F32, name="bank")
+            bank_b = sums.tile([PARTS, 2, HALVES, PARTS], F32, name="bank")
+            fours = [
+                [pixels[c][:, q, p, half * PARTS : (half + 1) * PARTS] for p in range(SIDE)] for half in range(HALVES)
+            ]
+            sums_of_two(nc, bank_a, bank_b, fours, ident[:])
+            odd = small.tile([PARTS, LANE], F32, name="odd")
+            signed_sums(nc, bank_a, bank_b, odd[:], rows[c][:, 0, q, :], rows[c][:, 1, q, :], rows[c][:, 2:4, q, :])
 
-        def column_stage(c, group):
-            if group == 0:
+        def column_stage(c, u):
+            if u == 0:
                 gy_grouped[c] = grouped.tile([PARTS, T, LANE], BF16, name="gy_grouped", align_bytes=64)
-            half, u = group // SIDE, group % SIDE
-            lane = slice(half * PARTS, (half + 1) * PARTS)
             t = SIDE * u
-            bank = sums.tile([PARTS, SIDE, PARTS], F32, name="bank")
-            sums_of_two(nc, bank, [rows[c][:, half, u, q, :] for q in range(SIDE)], ident[:])
-            odd = small.tile([PARTS, PARTS], F32, name="odd")
-            total = small.tile([PARTS, PARTS], F32, name="total")
-            signed_sums(
-                nc, bank, odd[:], total[:], gy_grouped[c][:, t + 1, lane], gy_grouped[c][:, t + 2 : t + 4, lane]
-            )
-            totals[group] = total
-            if group > 0:
-                round_total(c, group - 1)
+            bank_a = sums.tile([PARTS, 2, HALVES, PARTS], F32, name="bank")
+            bank_b = sums.tile([PARTS, 2, HALVES, PARTS], F32, name="bank")
+            fours = [
+                [rows[c][:, u, q, half * PARTS : (half + 1) * PARTS] for q in range(SIDE)] for half in range(HALVES)
+            ]
+            sums_of_two(nc, bank_a, bank_b, fours, ident[:])
+            odd = small.tile([PARTS, LANE], F32, name="odd")
+            total = small.tile([PARTS, LANE], F32, name="total")
+            signed_sums(nc, bank_a, bank_b, odd[:], total[:], gy_grouped[c][:, t + 1, :], gy_grouped[c][:, t + 2 : t + 4, :])
+            totals[u] = total
+            if u > 0:
+                round_total(c, u - 1)
 
-        def round_total(c, group):
-            half, u = group // SIDE, group % SIDE
-            lane = slice(half * PARTS, (half + 1) * PARTS)
-            nc.scalar.copy(out=gy_grouped[c][:, SIDE * u, lane], in_=totals[group][:])
+        def round_total(c, u):
+            nc.scalar.copy(out=gy_grouped[c][:, SIDE * u, :], in_=totals[u][:])
 
         def quantise(c):
-            round_total(c, GROUPS - 1)
+            round_total(c, SIDE - 1)
             x_codes = packed.tile([PARTS, COLS], U32, name="x_codes", align_bytes=64)
             x_scales = packed.tile([PARTS, COLS], U8, name="x_scales", align_bytes=64)
             nc.vector.quantize_mx(
@@ -204,16 +205,17 @@ def tile_iwht3layer_pa_k_kernel(tc, trans, weight, bias, grad_out, out):
             if c + 3 < PASSES:
                 load(c + 3)
             if c + 1 < PASSES:
-                for group in range(GROUPS):
-                    row_stage(c + 1, group)
-                    regroup(c + 1, group)
-                    if c + 2 < PASSES:
-                        widen(c + 2, group)
+                for q in range(SIDE):
+                    row_stage(c + 1, q)
+                    for piece in (2 * q, 2 * q + 1):
+                        regroup(c + 1, piece)
+                        if c + 2 < PASSES:
+                            widen(c + 2, piece)
             if c >= ROUND and c % ROUND == 0:
                 multiply(c - ROUND)
             if c >= 0:
-                for group in range(GROUPS):
-                    column_stage(c, group)
+                for u in range(SIDE):
+                    column_stage(c, u)
                 quantise(c)
         multiply(PASSES - ROUND)
 

@@ -12,6 +12,7 @@ E5M2_X4 = mybir.dt.float8_e5m2_x4
 ADD = mybir.AluOpType.add
 SUB = mybir.AluOpType.subtract
 MULT = mybir.AluOpType.mult
+COPY = mybir.ActivationFunctionType.Copy
 
 PARTS = 128
 PACK = 4
@@ -24,10 +25,12 @@ PASSES = N // K_PASS
 ROWS_PER_PASS = K_PASS // NW
 PARTS_PER_ROW = NW // PACK
 COLS = T * K
-ELEMS = COLS * PACK
 LANE = K * PACK
 HALVES = LANE // PARTS
-GROUPS = SIDE * HALVES
+K_HALF = K // HALVES
+CHUNKS = SIDE * HALVES
+STEPS = 4
+PIECES = 8
 
 M_TILE = 128
 N_TILE = 512
@@ -40,31 +43,8 @@ FLOPS = 2 * T * C * K * N + 4 * T * N * K
 BYTES = 2 * T * N * C + 2 * T * N * K + 4 * T * C * K
 
 
-def sums_of_two(nc, bank_a, bank_b, fours, ident):
-    for bank, pairs in ((bank_a, ((0, 2), (1, 3))), (bank_b, ((0, 1), (0, 3)))):
-        for place, (first, second) in enumerate(pairs):
-            for h, four in enumerate(fours):
-                nc.tensor.matmul(
-                    out=bank[:, place, h, :], lhsT=four[first], rhs=ident, is_transpose=True, start=True, stop=False
-                )
-                nc.tensor.matmul(
-                    out=bank[:, place, h, :], lhsT=four[second], rhs=ident, is_transpose=True, start=False, stop=True
-                )
-
-
-def signed_sums(nc, bank_a, bank_b, odd, out0, out1, out23):
-    even = bank_a[:, 0, :, :].rearrange("a h e -> a (h e)")
-    nc.scalar.copy(out=odd, in_=bank_a[:, 1, :, :].rearrange("a h e -> a (h e)"))
-    nc.vector.tensor_tensor(out=out0, in0=even, in1=odd, op=ADD)
-    nc.vector.tensor_tensor(out=out1, in0=even, in1=odd, op=SUB)
-    nc.vector.scalar_tensor_tensor(
-        out=out23,
-        in0=bank_b[:].rearrange("a u h e -> a u (h e)"),
-        scalar=2.0,
-        in1=out0.unsqueeze(1).to_broadcast([PARTS, 2, LANE]),
-        op0=MULT,
-        op1=SUB,
-    )
+def turn(nc, out, tile, moving, start, stop):
+    nc.tensor.matmul(out=out, lhsT=tile, rhs=moving, is_transpose=True, start=start, stop=stop)
 
 
 def tile_iwht3layer_pa_k_kernel(tc, trans, weight, bias, grad_out, out):
@@ -90,55 +70,65 @@ def tile_iwht3layer_pa_k_kernel(tc, trans, weight, bias, grad_out, out):
 
         ident = const.tile([PARTS, PARTS], F32)
         make_identity(nc, ident[:])
+        weave = const.tile([PARTS, PARTS], F32)
+        nc.vector.tensor_copy(
+            out=weave[:].rearrange("a (kk tau) -> a kk tau", tau=PACK),
+            in_=ident[:].rearrange("a (tau kk) -> a kk tau", tau=PACK),
+        )
         result = const.tile([M_TILE, PAIRS, M_TILE], F32)
 
-        g_raw, x_raw, pixels, rows, x_grouped, gy_grouped, codes = {}, {}, {}, {}, {}, {}, {}
-        totals = {}
+        g_raw, x_raw, first, rows, x_grouped, gy_grouped = {}, {}, {}, {}, {}, {}
+        x_packed, gy_packed, totals = {}, {}, {}
 
-        def load(c):
+        def load_g(c):
             g_raw[c] = raw.tile([PARTS, SIDE, SIDE * LANE], BF16, name="g_raw")
             for p in range(SIDE):
                 nc.sync.dma_start(out=g_raw[c][:, p, :], in_=g_dram[c, p])
+
+        def load_x(c):
             x_raw[c] = raw.tile([PARTS, T, LANE], BF16, name="x_raw")
             nc.sync.dma_start(out=x_raw[c][:], in_=x_dram[c])
 
-        def widen(c, piece):
-            if piece == 0:
-                pixels[c] = stages.tile([PARTS, SIDE, SIDE, LANE], F32, name="pixels")
-            q, first_p = piece // 2, 2 * (piece % 2)
-            nc.scalar.activation(
-                out=pixels[c][:, q, first_p : first_p + 2, :].rearrange("a p (k tau) -> a p k tau", tau=PACK),
-                in_=g_raw[c][:].rearrange("a p (tau q k) -> a q p k tau", tau=PACK, q=SIDE)[
-                    :, q, first_p : first_p + 2
-                ],
-                func=mybir.ActivationFunctionType.Copy,
-                scale=1.0 / T,
+        def first_level(engine, c, step):
+            if step == 0:
+                first[c] = stages.tile([PARTS, 2, 2, CHUNKS, PARTS], F32, name="first")
+            u0, p1 = step // 2, step % 2
+            upper, lower = [
+                g_raw[c][:, 2 * p1 + p0, :].rearrange("a (tau qh kk) -> a qh tau kk", tau=PACK, qh=CHUNKS)
+                for p0 in range(2)
+            ]
+            engine.tensor_tensor(
+                out=first[c][:, u0, p1, :, :].rearrange("a qh (tau kk) -> a qh tau kk", tau=PACK),
+                in0=upper,
+                in1=lower,
+                op=ADD if u0 == 0 else SUB,
             )
 
         def regroup(c, piece):
             if piece == 0:
                 x_grouped[c] = grouped.tile([PARTS, T, LANE], BF16, name="x_grouped", align_bytes=64)
             first_t = 2 * piece
-            nc.gpsimd.tensor_scalar(
+            nc.scalar.copy(
                 out=x_grouped[c][:, first_t : first_t + 2, :].rearrange("a t (c tau) -> a t c tau", tau=PACK),
-                in0=x_raw[c][:, first_t : first_t + 2, :].rearrange("a t (tau c) -> a t c tau", tau=PACK),
-                scalar1=1.0,
-                scalar2=0.0,
-                op0=MULT,
-                op1=ADD,
+                in_=x_raw[c][:, first_t : first_t + 2, :].rearrange("a t (tau c) -> a t c tau", tau=PACK),
             )
 
-        def row_stage(c, q):
-            if q == 0:
-                rows[c] = stages.tile([PARTS, SIDE, SIDE, LANE], F32, name="rows")
-            bank_a = sums.tile([PARTS, 2, HALVES, PARTS], F32, name="bank")
-            bank_b = sums.tile([PARTS, 2, HALVES, PARTS], F32, name="bank")
-            fours = [
-                [pixels[c][:, q, p, half * PARTS : (half + 1) * PARTS] for p in range(SIDE)] for half in range(HALVES)
-            ]
-            sums_of_two(nc, bank_a, bank_b, fours, ident[:])
-            odd = small.tile([PARTS, LANE], F32, name="odd")
-            signed_sums(nc, bank_a, bank_b, odd[:], rows[c][:, 0, q, :], rows[c][:, 1, q, :], rows[c][:, 2:4, q, :])
+        def pair_stage(c, step):
+            if step == 0:
+                rows[c] = stages.tile([PARTS, 2, 2, CHUNKS, PARTS], F32, name="rows")
+            u0, j = step // 2, step % 2
+            both = sums.tile([PARTS, 4, PARTS], F32, name="bank")
+            lone = sums.tile([PARTS, 4, PARTS], F32, name="bank")
+            for place in range(4):
+                turn(nc, both[:, place, :], first[c][:, u0, 0, 4 * j + place, :], ident[:], True, False)
+                turn(nc, both[:, place, :], first[c][:, u0, 1, 4 * j + place, :], ident[:], False, True)
+            for place in range(4):
+                turn(nc, lone[:, place, :], first[c][:, u0, 0, 4 * j + place, :], ident[:], True, True)
+            plus = rows[c][:, 0, u0, 4 * j : 4 * j + 4, :]
+            nc.scalar.activation(out=plus, in_=both[:], func=COPY, scale=1.0 / T)
+            nc.vector.scalar_tensor_tensor(
+                out=rows[c][:, 1, u0, 4 * j : 4 * j + 4, :], in0=lone[:], scalar=2.0 / T, in1=plus, op0=MULT, op1=SUB
+            )
 
         def column_stage(c, u):
             if u == 0:
@@ -146,33 +136,45 @@ def tile_iwht3layer_pa_k_kernel(tc, trans, weight, bias, grad_out, out):
             t = SIDE * u
             bank_a = sums.tile([PARTS, 2, HALVES, PARTS], F32, name="bank")
             bank_b = sums.tile([PARTS, 2, HALVES, PARTS], F32, name="bank")
-            fours = [
-                [rows[c][:, u, q, half * PARTS : (half + 1) * PARTS] for q in range(SIDE)] for half in range(HALVES)
-            ]
-            sums_of_two(nc, bank_a, bank_b, fours, ident[:])
+            for bank, pairs in ((bank_a, ((0, 2), (1, 3))), (bank_b, ((0, 1), (0, 3)))):
+                for place, (one, two) in enumerate(pairs):
+                    for half in range(HALVES):
+                        turn(nc, bank[:, place, half, :], rows[c][:, u // 2, u % 2, HALVES * one + half, :], weave[:], True, False)
+                        turn(nc, bank[:, place, half, :], rows[c][:, u // 2, u % 2, HALVES * two + half, :], weave[:], False, True)
             odd = small.tile([PARTS, LANE], F32, name="odd")
             total = small.tile([PARTS, LANE], F32, name="total")
-            signed_sums(nc, bank_a, bank_b, odd[:], total[:], gy_grouped[c][:, t + 1, :], gy_grouped[c][:, t + 2 : t + 4, :])
+            even = bank_a[:, 0, :, :].rearrange("a h e -> a (h e)")
+            nc.scalar.copy(out=odd[:], in_=bank_a[:, 1, :, :].rearrange("a h e -> a (h e)"))
+            nc.vector.tensor_tensor(out=total[:], in0=even, in1=odd[:], op=ADD)
+            nc.vector.tensor_tensor(out=gy_grouped[c][:, t + 1, :], in0=even, in1=odd[:], op=SUB)
+            nc.vector.scalar_tensor_tensor(
+                out=gy_grouped[c][:, t + 2 : t + 4, :],
+                in0=bank_b[:].rearrange("a v h e -> a v (h e)"),
+                scalar=2.0,
+                in1=total[:].unsqueeze(1).to_broadcast([PARTS, 2, LANE]),
+                op0=MULT,
+                op1=SUB,
+            )
             totals[u] = total
-            if u > 0:
-                round_total(c, u - 1)
 
         def round_total(c, u):
             nc.scalar.copy(out=gy_grouped[c][:, SIDE * u, :], in_=totals[u][:])
 
-        def quantise(c):
-            round_total(c, SIDE - 1)
-            x_codes = packed.tile([PARTS, COLS], U32, name="x_codes", align_bytes=64)
-            x_scales = packed.tile([PARTS, COLS], U8, name="x_scales", align_bytes=64)
+        def quantise_x(c):
+            codes = packed.tile([PARTS, COLS], U32, name="x_codes", align_bytes=64)
+            scales = packed.tile([PARTS, COLS], U8, name="x_scales", align_bytes=64)
             nc.vector.quantize_mx(
-                out=x_codes[:].bitcast(E4M3_X4), scales=x_scales[:], in_=x_grouped[c][:].rearrange("a t e -> a (t e)")
+                out=codes[:].bitcast(E4M3_X4), scales=scales[:], in_=x_grouped[c][:].rearrange("a t e -> a (t e)")
             )
-            gy_codes = packed.tile([PARTS, COLS], U32, name="gy_codes", align_bytes=64)
-            gy_scales = packed.tile([PARTS, COLS], U8, name="gy_scales", align_bytes=64)
+            x_packed[c] = (codes, scales)
+
+        def quantise_gy(c):
+            codes = packed.tile([PARTS, COLS], U32, name="gy_codes", align_bytes=64)
+            scales = packed.tile([PARTS, COLS], U8, name="gy_scales", align_bytes=64)
             nc.vector.quantize_mx(
-                out=gy_codes[:].bitcast(E5M2_X4), scales=gy_scales[:], in_=gy_grouped[c][:].rearrange("a t e -> a (t e)")
+                out=codes[:].bitcast(E5M2_X4), scales=scales[:], in_=gy_grouped[c][:].rearrange("a t e -> a (t e)")
             )
-            codes[c] = (x_codes, x_scales, gy_codes, gy_scales)
+            gy_packed[c] = (codes, scales)
 
         def multiply(first_pass):
             for s in range(PAIRS):
@@ -181,13 +183,12 @@ def tile_iwht3layer_pa_k_kernel(tc, trans, weight, bias, grad_out, out):
                 n_cols = slice(n_first, n_first + N_TILE)
                 product = products.tile([M_TILE, N_TILE], F32, name="product")
                 for c in range(first_pass, first_pass + ROUND):
-                    x_codes, x_scales, gy_codes, gy_scales = codes[c]
                     nc.tensor.matmul_mx(
                         out=product[:],
-                        lhsT=x_codes[:, m_cols].bitcast(E4M3_X4),
-                        lhsT_scale=x_scales[:, m_cols],
-                        rhs=gy_codes[:, n_cols].bitcast(E5M2_X4),
-                        rhs_scale=gy_scales[:, n_cols],
+                        lhsT=x_packed[c][0][:, m_cols].bitcast(E4M3_X4),
+                        lhsT_scale=x_packed[c][1][:, m_cols],
+                        rhs=gy_packed[c][0][:, n_cols].bitcast(E5M2_X4),
+                        rhs_scale=gy_packed[c][1][:, n_cols],
                         start=(c == first_pass),
                         stop=(c == first_pass + ROUND - 1),
                     )
@@ -197,26 +198,41 @@ def tile_iwht3layer_pa_k_kernel(tc, trans, weight, bias, grad_out, out):
                 else:
                     nc.vector.tensor_tensor(out=result[:, s, :], in0=product[:, wanted], in1=result[:, s, :], op=ADD)
 
-        load(0)
-        load(1)
-        for piece in range(GROUPS):
-            widen(0, piece)
+        load_g(0)
+        load_g(1)
+        load_x(0)
+        load_g(2)
+        load_x(1)
+        for step in range(STEPS):
+            first_level(nc.vector, 0, step)
+        for step in range(STEPS):
+            first_level(nc.gpsimd, 1, step)
         for c in range(-1, PASSES):
             if c + 3 < PASSES:
-                load(c + 3)
-            if c + 1 < PASSES:
-                for q in range(SIDE):
-                    row_stage(c + 1, q)
-                    for piece in (2 * q, 2 * q + 1):
-                        regroup(c + 1, piece)
-                        if c + 2 < PASSES:
-                            widen(c + 2, piece)
+                load_g(c + 3)
+            if c + 2 < PASSES:
+                load_x(c + 2)
+            for step in range(STEPS):
+                if 0 <= c and c + 2 < PASSES:
+                    first_level(nc.gpsimd, c + 2, step)
+                if c + 1 < PASSES:
+                    pair_stage(c + 1, step)
+                if c >= 0:
+                    column_stage(c, step)
+                    if step > 0:
+                        round_total(c, step - 1)
+                if c + 1 < PASSES:
+                    regroup(c + 1, 2 * step)
+                    regroup(c + 1, 2 * step + 1)
+                if step == 0 and c >= 1:
+                    quantise_gy(c - 1)
+                if step == 2 and c >= 0:
+                    quantise_x(c)
+            if c >= 0:
+                round_total(c, STEPS - 1)
             if c >= ROUND and c % ROUND == 0:
                 multiply(c - ROUND)
-            if c >= 0:
-                for u in range(SIDE):
-                    column_stage(c, u)
-                quantise(c)
+        quantise_gy(PASSES - 1)
         multiply(PASSES - ROUND)
 
         out_view = out.rearrange("(s two) c k -> two c s k", two=T_PER_M)

@@ -63,7 +63,7 @@ def tile_iwht3layer_pa_k_kernel(tc, trans, weight, bias, grad_out, out):
         raw = ctx.enter_context(tc.tile_pool(name="raw", bufs=3))
         stages = ctx.enter_context(tc.tile_pool(name="stages", bufs=2))
         small = ctx.enter_context(tc.tile_pool(name="small", bufs=4))
-        grouped = ctx.enter_context(tc.tile_pool(name="grouped", bufs=2))
+        grouped = ctx.enter_context(tc.tile_pool(name="grouped", bufs=3))
         packed = ctx.enter_context(tc.tile_pool(name="packed", bufs=4))
         sums = ctx.enter_context(tc.psum_pool(name="sums", bufs=6))
         products = ctx.enter_context(tc.psum_pool(name="products", bufs=2))
@@ -176,6 +176,10 @@ def tile_iwht3layer_pa_k_kernel(tc, trans, weight, bias, grad_out, out):
             )
             gy_packed[c] = (codes, scales)
 
+        def hold_gpsimd(c):
+            junk = small.tile([PARTS, 16], U32, name="junk")
+            nc.gpsimd.tensor_copy(out=junk[:], in_=gy_packed[c][0][:, 0:16])
+
         def multiply(first_pass):
             for s in range(PAIRS):
                 m_cols = slice(s * M_TILE, (s + 1) * M_TILE)
@@ -224,15 +228,14 @@ def tile_iwht3layer_pa_k_kernel(tc, trans, weight, bias, grad_out, out):
                 if c + 1 < PASSES:
                     regroup(c + 1, 2 * step)
                     regroup(c + 1, 2 * step + 1)
-                if step == 0 and c >= 1:
-                    quantise_gy(c - 1)
-                if step == 2 and c >= 0:
-                    quantise_x(c)
+                if step == 2 and c >= ROUND and c % ROUND == 0:
+                    multiply(c - ROUND)
             if c >= 0:
                 round_total(c, STEPS - 1)
-            if c >= ROUND and c % ROUND == 0:
-                multiply(c - ROUND)
-        quantise_gy(PASSES - 1)
+                quantise_x(c)
+                quantise_gy(c)
+                if c + 3 < PASSES:
+                    hold_gpsimd(c)
         multiply(PASSES - ROUND)
 
         out_view = out.rearrange("(s two) c k -> two c s k", two=T_PER_M)

@@ -37,7 +37,7 @@ N_TILE = 512
 T_PER_M = M_TILE // C
 T_PER_N = N_TILE // K
 PAIRS = T // T_PER_M
-ROUND = 2
+LEAD = 2
 
 FLOPS = 2 * T * C * K * N + 4 * T * N * K
 BYTES = 2 * T * N * C + 2 * T * N * K + 4 * T * C * K
@@ -79,6 +79,7 @@ def tile_iwht3layer_pa_k_kernel(tc, trans, weight, bias, grad_out, out):
 
         g_raw, x_raw, first, rows, x_grouped, gy_grouped = {}, {}, {}, {}, {}, {}
         x_packed, gy_packed, totals = {}, {}, {}
+        started = set()
 
         def load_g(c):
             g_raw[c] = raw.tile([PARTS, SIDE, SIDE * LANE], BF16, name="g_raw")
@@ -113,49 +114,72 @@ def tile_iwht3layer_pa_k_kernel(tc, trans, weight, bias, grad_out, out):
                 in_=x_raw[c][:, first_t : first_t + 2, :].rearrange("a t (tau c) -> a t c tau", tau=PACK),
             )
 
-        def pair_stage(c, step):
-            if step == 0:
-                rows[c] = stages.tile([PARTS, 2, 2, CHUNKS, PARTS], F32, name="rows")
+        def pair_unit(c, step):
             u0, j = step // 2, step % 2
-            both = sums.tile([PARTS, 4, PARTS], F32, name="bank")
-            lone = sums.tile([PARTS, 4, PARTS], F32, name="bank")
-            for place in range(4):
-                turn(nc, both[:, place, :], first[c][:, u0, 0, 4 * j + place, :], ident[:], True, False)
-                turn(nc, both[:, place, :], first[c][:, u0, 1, 4 * j + place, :], ident[:], False, True)
-            for place in range(4):
-                turn(nc, lone[:, place, :], first[c][:, u0, 0, 4 * j + place, :], ident[:], True, True)
-            plus = rows[c][:, 0, u0, 4 * j : 4 * j + 4, :]
-            nc.scalar.activation(out=plus, in_=both[:], func=COPY, scale=1.0 / T)
-            nc.vector.scalar_tensor_tensor(
-                out=rows[c][:, 1, u0, 4 * j : 4 * j + 4, :], in0=lone[:], scalar=2.0 / T, in1=plus, op0=MULT, op1=SUB
-            )
+            banks = {}
 
-        def column_stage(c, u):
-            if u == 0:
-                gy_grouped[c] = grouped.tile([PARTS, T, LANE], BF16, name="gy_grouped", align_bytes=64)
+            def fill():
+                banks["both"] = sums.tile([PARTS, 4, PARTS], F32, name="bank")
+                banks["lone"] = sums.tile([PARTS, 4, PARTS], F32, name="bank")
+                for place in range(4):
+                    turn(nc, banks["both"][:, place, :], first[c][:, u0, 0, 4 * j + place, :], ident[:], True, False)
+                    turn(nc, banks["both"][:, place, :], first[c][:, u0, 1, 4 * j + place, :], ident[:], False, True)
+                for place in range(4):
+                    turn(nc, banks["lone"][:, place, :], first[c][:, u0, 0, 4 * j + place, :], ident[:], True, True)
+
+            def empty():
+                if step == 0:
+                    rows[c] = stages.tile([PARTS, 2, 2, CHUNKS, PARTS], F32, name="rows")
+                plus = rows[c][:, 0, u0, 4 * j : 4 * j + 4, :]
+                nc.scalar.activation(out=plus, in_=banks["both"][:], func=COPY, scale=1.0 / T)
+                nc.vector.scalar_tensor_tensor(
+                    out=rows[c][:, 1, u0, 4 * j : 4 * j + 4, :],
+                    in0=banks["lone"][:],
+                    scalar=2.0 / T,
+                    in1=plus,
+                    op0=MULT,
+                    op1=SUB,
+                )
+                regroup(c, 2 * step)
+                regroup(c, 2 * step + 1)
+
+            return fill, empty
+
+        def column_unit(c, u):
             t = SIDE * u
-            bank_a = sums.tile([PARTS, 2, HALVES, PARTS], F32, name="bank")
-            bank_b = sums.tile([PARTS, 2, HALVES, PARTS], F32, name="bank")
-            for bank, pairs in ((bank_a, ((0, 2), (1, 3))), (bank_b, ((0, 1), (0, 3)))):
-                for place, (one, two) in enumerate(pairs):
-                    for half in range(HALVES):
-                        turn(nc, bank[:, place, half, :], rows[c][:, u // 2, u % 2, HALVES * one + half, :], weave[:], True, False)
-                        turn(nc, bank[:, place, half, :], rows[c][:, u // 2, u % 2, HALVES * two + half, :], weave[:], False, True)
-            odd = small.tile([PARTS, LANE], F32, name="odd")
-            total = small.tile([PARTS, LANE], F32, name="total")
-            even = bank_a[:, 0, :, :].rearrange("a h e -> a (h e)")
-            nc.scalar.copy(out=odd[:], in_=bank_a[:, 1, :, :].rearrange("a h e -> a (h e)"))
-            nc.vector.tensor_tensor(out=total[:], in0=even, in1=odd[:], op=ADD)
-            nc.vector.tensor_tensor(out=gy_grouped[c][:, t + 1, :], in0=even, in1=odd[:], op=SUB)
-            nc.vector.scalar_tensor_tensor(
-                out=gy_grouped[c][:, t + 2 : t + 4, :],
-                in0=bank_b[:].rearrange("a v h e -> a v (h e)"),
-                scalar=2.0,
-                in1=total[:].unsqueeze(1).to_broadcast([PARTS, 2, LANE]),
-                op0=MULT,
-                op1=SUB,
-            )
-            totals[u] = total
+            banks = {}
+
+            def fill():
+                banks["a"] = sums.tile([PARTS, 2, HALVES, PARTS], F32, name="bank")
+                banks["b"] = sums.tile([PARTS, 2, HALVES, PARTS], F32, name="bank")
+                for bank, pairs in ((banks["a"], ((0, 2), (1, 3))), (banks["b"], ((0, 1), (0, 3)))):
+                    for place, (one, two) in enumerate(pairs):
+                        for half in range(HALVES):
+                            turn(nc, bank[:, place, half, :], rows[c][:, u // 2, u % 2, HALVES * one + half, :], weave[:], True, False)
+                            turn(nc, bank[:, place, half, :], rows[c][:, u // 2, u % 2, HALVES * two + half, :], weave[:], False, True)
+
+            def empty():
+                if u == 0:
+                    gy_grouped[c] = grouped.tile([PARTS, T, LANE], BF16, name="gy_grouped", align_bytes=64)
+                odd = small.tile([PARTS, LANE], F32, name="odd")
+                total = small.tile([PARTS, LANE], F32, name="total")
+                even = banks["a"][:, 0, :, :].rearrange("a h e -> a (h e)")
+                nc.scalar.copy(out=odd[:], in_=banks["a"][:, 1, :, :].rearrange("a h e -> a (h e)"))
+                nc.vector.tensor_tensor(out=total[:], in0=even, in1=odd[:], op=ADD)
+                nc.vector.tensor_tensor(out=gy_grouped[c][:, t + 1, :], in0=even, in1=odd[:], op=SUB)
+                nc.vector.scalar_tensor_tensor(
+                    out=gy_grouped[c][:, t + 2 : t + 4, :],
+                    in0=banks["b"][:].rearrange("a v h e -> a v (h e)"),
+                    scalar=2.0,
+                    in1=total[:].unsqueeze(1).to_broadcast([PARTS, 2, LANE]),
+                    op0=MULT,
+                    op1=SUB,
+                )
+                totals[u] = total
+                if u > 0:
+                    round_total(c, u - 1)
+
+            return fill, empty
 
         def round_total(c, u):
             nc.scalar.copy(out=gy_grouped[c][:, SIDE * u, :], in_=totals[u][:])
@@ -180,63 +204,79 @@ def tile_iwht3layer_pa_k_kernel(tc, trans, weight, bias, grad_out, out):
             junk = small.tile([PARTS, 16], U32, name="junk")
             nc.gpsimd.tensor_copy(out=junk[:], in_=gy_packed[c][0][:, 0:16])
 
-        def multiply(first_pass):
-            for s in range(PAIRS):
-                m_cols = slice(s * M_TILE, (s + 1) * M_TILE)
-                n_first = (s * T_PER_M // T_PER_N) * N_TILE
-                n_cols = slice(n_first, n_first + N_TILE)
-                product = products.tile([M_TILE, N_TILE], F32, name="product")
-                for c in range(first_pass, first_pass + ROUND):
-                    nc.tensor.matmul_mx(
-                        out=product[:],
-                        lhsT=x_packed[c][0][:, m_cols].bitcast(E4M3_X4),
-                        lhsT_scale=x_packed[c][1][:, m_cols],
-                        rhs=gy_packed[c][0][:, n_cols].bitcast(E5M2_X4),
-                        rhs_scale=gy_packed[c][1][:, n_cols],
-                        start=(c == first_pass),
-                        stop=(c == first_pass + ROUND - 1),
-                    )
-                wanted = slice(s * M_TILE - n_first, (s + 1) * M_TILE - n_first)
-                if first_pass == 0:
-                    nc.vector.tensor_copy(out=result[:, s, :], in_=product[:, wanted])
-                else:
-                    nc.vector.tensor_tensor(out=result[:, s, :], in0=product[:, wanted], in1=result[:, s, :], op=ADD)
+        def product(s, passes):
+            m_cols = slice(s * M_TILE, (s + 1) * M_TILE)
+            n_first = (s * T_PER_M // T_PER_N) * N_TILE
+            n_cols = slice(n_first, n_first + N_TILE)
+            bank = products.tile([M_TILE, N_TILE], F32, name="product")
+            for c in passes:
+                nc.tensor.matmul_mx(
+                    out=bank[:],
+                    lhsT=x_packed[c][0][:, m_cols].bitcast(E4M3_X4),
+                    lhsT_scale=x_packed[c][1][:, m_cols],
+                    rhs=gy_packed[c][0][:, n_cols].bitcast(E5M2_X4),
+                    rhs_scale=gy_packed[c][1][:, n_cols],
+                    start=(c == passes[0]),
+                    stop=(c == passes[-1]),
+                )
+            return bank
+
+        def collect(s, bank):
+            n_first = (s * T_PER_M // T_PER_N) * N_TILE
+            wanted = slice(s * M_TILE - n_first, (s + 1) * M_TILE - n_first)
+            if s in started:
+                nc.vector.tensor_tensor(out=result[:, s, :], in0=bank[:, wanted], in1=result[:, s, :], op=ADD)
+            else:
+                nc.vector.tensor_copy(out=result[:, s, :], in_=bank[:, wanted])
+                started.add(s)
+
+        def window(c):
+            round_total(c, SIDE - 1)
+            passes = [done for done in (c - 2, c - 1) if done >= 0]
+            half = [4 * (c % 2) + i for i in range(4)] if passes else []
+            made = [(s, product(s, passes)) for s in half[:2]]
+            quantise_x(c)
+            for s, bank in made:
+                collect(s, bank)
+            made = [(s, product(s, passes)) for s in half[2:]]
+            quantise_gy(c)
+            for s, bank in made:
+                collect(s, bank)
+            if c + 3 < PASSES:
+                hold_gpsimd(c)
+
+        units = []
+        for c in range(-1, PASSES):
+            for step in range(STEPS):
+                if c + 1 < PASSES:
+                    units.append(("pair", c + 1, step) + pair_unit(c + 1, step))
+                if c >= 0:
+                    units.append(("column", c, step) + column_unit(c, step))
 
         load_g(0)
         load_g(1)
         load_x(0)
-        load_g(2)
-        load_x(1)
         for step in range(STEPS):
             first_level(nc.vector, 0, step)
         for step in range(STEPS):
             first_level(nc.gpsimd, 1, step)
-        for c in range(-1, PASSES):
-            if c + 3 < PASSES:
-                load_g(c + 3)
-            if c + 2 < PASSES:
-                load_x(c + 2)
-            for step in range(STEPS):
-                if 0 <= c and c + 2 < PASSES:
-                    first_level(nc.gpsimd, c + 2, step)
-                if c + 1 < PASSES:
-                    pair_stage(c + 1, step)
-                if c >= 0:
-                    column_stage(c, step)
-                    if step > 0:
-                        round_total(c, step - 1)
-                if c + 1 < PASSES:
-                    regroup(c + 1, 2 * step)
-                    regroup(c + 1, 2 * step + 1)
-                if step == 2 and c >= ROUND and c % ROUND == 0:
-                    multiply(c - ROUND)
-            if c >= 0:
-                round_total(c, STEPS - 1)
-                quantise_x(c)
-                quantise_gy(c)
-                if c + 3 < PASSES:
-                    hold_gpsimd(c)
-        multiply(PASSES - ROUND)
+        for ahead in range(LEAD):
+            units[ahead][3]()
+        for i, (kind, c, step, fill, empty) in enumerate(units):
+            if kind == "pair":
+                if step == 0 and c + 2 < PASSES:
+                    load_g(c + 2)
+                if step == 0 and c + 1 < PASSES:
+                    load_x(c + 1)
+                if c >= 1 and c + 1 < PASSES:
+                    first_level(nc.gpsimd, c + 1, step)
+            if i + LEAD < len(units):
+                units[i + LEAD][3]()
+            empty()
+            if kind == "column" and step == STEPS - 1:
+                window(c)
+        for s in range(PAIRS):
+            collect(s, product(s, [PASSES - 2, PASSES - 1] if s < 4 else [PASSES - 1]))
 
         out_view = out.rearrange("(s two) c k -> two c s k", two=T_PER_M)
         nc.sync.dma_start(out=out_view[0], in_=result[0:C, :, 0:K])

@@ -64,7 +64,7 @@ def tile_iwht3layer_pa_k_kernel(tc, trans, weight, bias, grad_out, out):
         stages = ctx.enter_context(tc.tile_pool(name="stages", bufs=2))
         small = ctx.enter_context(tc.tile_pool(name="small", bufs=4))
         grouped = ctx.enter_context(tc.tile_pool(name="grouped", bufs=3))
-        packed = ctx.enter_context(tc.tile_pool(name="packed", bufs=4))
+        packed = ctx.enter_context(tc.tile_pool(name="packed", bufs=5))
         sums = ctx.enter_context(tc.psum_pool(name="sums", bufs=6))
         products = ctx.enter_context(tc.psum_pool(name="products", bufs=2))
 
@@ -80,26 +80,26 @@ def tile_iwht3layer_pa_k_kernel(tc, trans, weight, bias, grad_out, out):
         g_raw, x_raw, first, rows, x_grouped, gy_grouped = {}, {}, {}, {}, {}, {}
         x_packed, gy_packed, totals = {}, {}, {}
         started = set()
+        seen = {}
 
         def load_g(c):
-            g_raw[c] = raw.tile([PARTS, SIDE, SIDE * LANE], BF16, name="g_raw")
+            g_raw[c] = raw.tile([PARTS, 2, 2, SIDE * LANE], BF16, name="g_raw")
             for p in range(SIDE):
-                nc.sync.dma_start(out=g_raw[c][:, p, :], in_=g_dram[c, p])
+                nc.sync.dma_start(out=g_raw[c][:, p % 2, p // 2, :], in_=g_dram[c, p])
 
         def load_x(c):
             x_raw[c] = raw.tile([PARTS, T, LANE], BF16, name="x_raw")
             nc.sync.dma_start(out=x_raw[c][:], in_=x_dram[c])
 
-        def first_level(engine, c, step):
-            if step == 0:
-                first[c] = stages.tile([PARTS, 2, 2, CHUNKS, PARTS], F32, name="first")
-            u0, p1 = step // 2, step % 2
+        def first_level(engine, c, u0):
+            if u0 == 0:
+                first[c] = stages.tile([PARTS, 2, CHUNKS, 2, PARTS], F32, name="first")
             upper, lower = [
-                g_raw[c][:, 2 * p1 + p0, :].rearrange("a (tau qh kk) -> a qh tau kk", tau=PACK, qh=CHUNKS)
+                g_raw[c][:, p0, :, :].rearrange("a p1 e -> a (p1 e)").rearrange("a (pt qh kk) -> a qh pt kk", pt=2 * PACK, qh=CHUNKS)
                 for p0 in range(2)
             ]
             engine.tensor_tensor(
-                out=first[c][:, u0, p1, :, :].rearrange("a qh (tau kk) -> a qh tau kk", tau=PACK),
+                out=first[c][:, u0, :, :, :].rearrange("a qh p1 e -> a (qh p1 e)").rearrange("a (qh pt kk) -> a qh pt kk", pt=2 * PACK, qh=CHUNKS),
                 in0=upper,
                 in1=lower,
                 op=ADD if u0 == 0 else SUB,
@@ -122,10 +122,10 @@ def tile_iwht3layer_pa_k_kernel(tc, trans, weight, bias, grad_out, out):
                 banks["both"] = sums.tile([PARTS, 4, PARTS], F32, name="bank")
                 banks["lone"] = sums.tile([PARTS, 4, PARTS], F32, name="bank")
                 for place in range(4):
-                    turn(nc, banks["both"][:, place, :], first[c][:, u0, 0, 4 * j + place, :], ident[:], True, False)
-                    turn(nc, banks["both"][:, place, :], first[c][:, u0, 1, 4 * j + place, :], ident[:], False, True)
+                    turn(nc, banks["both"][:, place, :], first[c][:, u0, 4 * j + place, 0, :], ident[:], True, False)
+                    turn(nc, banks["both"][:, place, :], first[c][:, u0, 4 * j + place, 1, :], ident[:], False, True)
                 for place in range(4):
-                    turn(nc, banks["lone"][:, place, :], first[c][:, u0, 0, 4 * j + place, :], ident[:], True, True)
+                    turn(nc, banks["lone"][:, place, :], first[c][:, u0, 4 * j + place, 0, :], ident[:], True, True)
 
             def empty():
                 if step == 0:
@@ -200,26 +200,23 @@ def tile_iwht3layer_pa_k_kernel(tc, trans, weight, bias, grad_out, out):
             )
             gy_packed[c] = (codes, scales)
 
-        def hold_gpsimd(c):
-            junk = small.tile([PARTS, 16], U32, name="junk")
-            nc.gpsimd.tensor_copy(out=junk[:], in_=gy_packed[c][0][:, 0:16])
+        def hold_gpsimd(written, dtype):
+            junk = small.tile([PARTS, 16], dtype, name="junk")
+            nc.gpsimd.tensor_copy(out=junk[:], in_=written)
 
-        def product(s, passes):
+        def mx_pass(bank, s, c, start, stop):
             m_cols = slice(s * M_TILE, (s + 1) * M_TILE)
             n_first = (s * T_PER_M // T_PER_N) * N_TILE
             n_cols = slice(n_first, n_first + N_TILE)
-            bank = products.tile([M_TILE, N_TILE], F32, name="product")
-            for c in passes:
-                nc.tensor.matmul_mx(
-                    out=bank[:],
-                    lhsT=x_packed[c][0][:, m_cols].bitcast(E4M3_X4),
-                    lhsT_scale=x_packed[c][1][:, m_cols],
-                    rhs=gy_packed[c][0][:, n_cols].bitcast(E5M2_X4),
-                    rhs_scale=gy_packed[c][1][:, n_cols],
-                    start=(c == passes[0]),
-                    stop=(c == passes[-1]),
-                )
-            return bank
+            nc.tensor.matmul_mx(
+                out=bank[:],
+                lhsT=x_packed[c][0][:, m_cols].bitcast(E4M3_X4),
+                lhsT_scale=x_packed[c][1][:, m_cols],
+                rhs=gy_packed[c][0][:, n_cols].bitcast(E5M2_X4),
+                rhs_scale=gy_packed[c][1][:, n_cols],
+                start=start,
+                stop=stop,
+            )
 
         def collect(s, bank):
             n_first = (s * T_PER_M // T_PER_N) * N_TILE
@@ -232,18 +229,26 @@ def tile_iwht3layer_pa_k_kernel(tc, trans, weight, bias, grad_out, out):
 
         def window(c):
             round_total(c, SIDE - 1)
-            passes = [done for done in (c - 2, c - 1) if done >= 0]
-            half = [4 * (c % 2) + i for i in range(4)] if passes else []
-            made = [(s, product(s, passes)) for s in half[:2]]
+            last = c == PASSES - 1
+            made = []
+            for s in range(PAIRS) if last else (2 * (c % 4), 2 * (c % 4) + 1):
+                passes = list(range(seen.get(s, 0), c))
+                if passes or last:
+                    pool = sums if last and s < 6 else products
+                    bank = pool.tile([M_TILE, N_TILE], F32, name="bank" if last and s < 6 else "product")
+                    for done in passes:
+                        mx_pass(bank, s, done, done == passes[0], done == passes[-1] and not last)
+                    made.append((s, bank, not passes))
+                    seen[s] = c
             quantise_x(c)
-            for s, bank in made:
-                collect(s, bank)
-            made = [(s, product(s, passes)) for s in half[2:]]
             quantise_gy(c)
-            for s, bank in made:
-                collect(s, bank)
             if c + 3 < PASSES:
-                hold_gpsimd(c)
+                hold_gpsimd(gy_packed[c][0][:, 0:16], U32)
+            for s, bank, fresh in made:
+                if last:
+                    mx_pass(bank, s, c, fresh, True)
+            for s, bank, fresh in made:
+                collect(s, bank)
 
         units = []
         for c in range(-1, PASSES):
@@ -256,10 +261,11 @@ def tile_iwht3layer_pa_k_kernel(tc, trans, weight, bias, grad_out, out):
         load_g(0)
         load_g(1)
         load_x(0)
-        for step in range(STEPS):
-            first_level(nc.vector, 0, step)
-        for step in range(STEPS):
-            first_level(nc.gpsimd, 1, step)
+        for u0 in range(2):
+            first_level(nc.vector, 0, u0)
+        hold_gpsimd(first[0][:, 1, CHUNKS - 1, 1, PARTS - 16 : PARTS], F32)
+        for u0 in range(2):
+            first_level(nc.gpsimd, 1, u0)
         for ahead in range(LEAD):
             units[ahead][3]()
         for i, (kind, c, step, fill, empty) in enumerate(units):
@@ -268,16 +274,14 @@ def tile_iwht3layer_pa_k_kernel(tc, trans, weight, bias, grad_out, out):
                     load_g(c + 2)
                 if step == 0 and c + 1 < PASSES:
                     load_x(c + 1)
-                if c >= 1 and c + 1 < PASSES:
-                    first_level(nc.gpsimd, c + 1, step)
+                if c >= 1 and c + 1 < PASSES and step % 2 == 0:
+                    first_level(nc.gpsimd, c + 1, step // 2)
             if i + LEAD < len(units):
                 units[i + LEAD][3]()
             empty()
             if kind == "column" and step == STEPS - 1:
                 window(c)
-        for s in range(PAIRS):
-            collect(s, product(s, [PASSES - 2, PASSES - 1] if s < 4 else [PASSES - 1]))
 
         out_view = out.rearrange("(s two) c k -> two c s k", two=T_PER_M)
         nc.sync.dma_start(out=out_view[0], in_=result[0:C, :, 0:K])
-        nc.sync.dma_start(out=out_view[1], in_=result[C:M_TILE, :, K:M_TILE])
+        nc.scalar.dma_start(out=out_view[1], in_=result[C:M_TILE, :, K:M_TILE])

@@ -65,8 +65,7 @@ def tile_iwht3layer_pa_k_kernel(tc, trans, weight, bias, grad_out, out):
         small = ctx.enter_context(tc.tile_pool(name="small", bufs=4))
         grouped = ctx.enter_context(tc.tile_pool(name="grouped", bufs=3))
         packed = ctx.enter_context(tc.tile_pool(name="packed", bufs=5))
-        sums = ctx.enter_context(tc.psum_pool(name="sums", bufs=6))
-        products = ctx.enter_context(tc.psum_pool(name="products", bufs=2))
+        sums = ctx.enter_context(tc.psum_pool(name="sums", bufs=8))
 
         ident = const.tile([PARTS, PARTS], F32)
         make_identity(nc, ident[:])
@@ -91,15 +90,17 @@ def tile_iwht3layer_pa_k_kernel(tc, trans, weight, bias, grad_out, out):
             x_raw[c] = raw.tile([PARTS, T, LANE], BF16, name="x_raw")
             nc.sync.dma_start(out=x_raw[c][:], in_=x_dram[c])
 
-        def first_level(engine, c, u0):
-            if u0 == 0:
+        def first_level(engine, c, u0, chunks):
+            if u0 == 0 and chunks.start == 0:
                 first[c] = stages.tile([PARTS, 2, CHUNKS, 2, PARTS], F32, name="first")
             upper, lower = [
-                g_raw[c][:, p0, :, :].rearrange("a p1 e -> a (p1 e)").rearrange("a (pt qh kk) -> a qh pt kk", pt=2 * PACK, qh=CHUNKS)
+                g_raw[c][:, p0, :, :].rearrange("a p1 e -> a (p1 e)").rearrange("a (pt qh kk) -> a qh pt kk", pt=2 * PACK, qh=CHUNKS)[
+                    :, chunks
+                ]
                 for p0 in range(2)
             ]
             engine.tensor_tensor(
-                out=first[c][:, u0, :, :, :].rearrange("a qh p1 e -> a (qh p1 e)").rearrange("a (qh pt kk) -> a qh pt kk", pt=2 * PACK, qh=CHUNKS),
+                out=first[c][:, u0, chunks, :, :].rearrange("a qh p1 e -> a (qh p1 e)").rearrange("a (qh pt kk) -> a qh pt kk", pt=2 * PACK, kk=K_HALF),
                 in0=upper,
                 in1=lower,
                 op=ADD if u0 == 0 else SUB,
@@ -192,13 +193,18 @@ def tile_iwht3layer_pa_k_kernel(tc, trans, weight, bias, grad_out, out):
             )
             x_packed[c] = (codes, scales)
 
-        def quantise_gy(c):
-            codes = packed.tile([PARTS, COLS], U32, name="gy_codes", align_bytes=64)
-            scales = packed.tile([PARTS, COLS], U8, name="gy_scales", align_bytes=64)
+        def quantise_gy(c, parts):
+            if c not in gy_packed:
+                codes = packed.tile([PARTS, COLS], U32, name="gy_codes", align_bytes=64)
+                scales = packed.tile([PARTS, COLS], U8, name="gy_scales", align_bytes=64)
+                gy_packed[c] = (codes, scales)
+            codes, scales = gy_packed[c]
+            cols = slice(parts[0] * COLS // 2, (parts[-1] + 1) * COLS // 2)
             nc.vector.quantize_mx(
-                out=codes[:].bitcast(E5M2_X4), scales=scales[:], in_=gy_grouped[c][:].rearrange("a t e -> a (t e)")
+                out=codes[:, cols].bitcast(E5M2_X4),
+                scales=scales[:, cols],
+                in_=gy_grouped[c][:, parts[0] * T // 2 : (parts[-1] + 1) * T // 2, :].rearrange("a t e -> a (t e)"),
             )
-            gy_packed[c] = (codes, scales)
 
         def hold_gpsimd(written, dtype):
             junk = small.tile([PARTS, 16], dtype, name="junk")
@@ -234,14 +240,13 @@ def tile_iwht3layer_pa_k_kernel(tc, trans, weight, bias, grad_out, out):
             for s in range(PAIRS) if last else (2 * (c % 4), 2 * (c % 4) + 1):
                 passes = list(range(seen.get(s, 0), c))
                 if passes or last:
-                    pool = sums if last and s < 6 else products
-                    bank = pool.tile([M_TILE, N_TILE], F32, name="bank" if last and s < 6 else "product")
+                    bank = sums.tile([M_TILE, N_TILE], F32, name="bank")
                     for done in passes:
                         mx_pass(bank, s, done, done == passes[0], done == passes[-1] and not last)
                     made.append((s, bank, not passes))
                     seen[s] = c
             quantise_x(c)
-            quantise_gy(c)
+            quantise_gy(c, (0, 1))
             if c + 3 < PASSES:
                 hold_gpsimd(gy_packed[c][0][:, 0:16], U32)
             for s, bank, fresh in made:
@@ -259,13 +264,14 @@ def tile_iwht3layer_pa_k_kernel(tc, trans, weight, bias, grad_out, out):
                     units.append(("column", c, step) + column_unit(c, step))
 
         load_g(0)
-        load_g(1)
         load_x(0)
+        load_g(1)
+        warm = const.tile([PARTS, 1], F32)
+        nc.vector.memset(warm[:], 0.0)
+        nc.scalar.activation(out=warm[:], in_=warm[:], func=COPY, scale=1.0)
         for u0 in range(2):
-            first_level(nc.vector, 0, u0)
-        hold_gpsimd(first[0][:, 1, CHUNKS - 1, 1, PARTS - 16 : PARTS], F32)
-        for u0 in range(2):
-            first_level(nc.gpsimd, 1, u0)
+            for j in range(2):
+                first_level(nc.vector, 0, u0, slice(4 * j, 4 * j + 4))
         for ahead in range(LEAD):
             units[ahead][3]()
         for i, (kind, c, step, fill, empty) in enumerate(units):
@@ -274,8 +280,13 @@ def tile_iwht3layer_pa_k_kernel(tc, trans, weight, bias, grad_out, out):
                     load_g(c + 2)
                 if step == 0 and c + 1 < PASSES:
                     load_x(c + 1)
+                if c == 0 and step < 2:
+                    first_level(nc.vector, 1, 0, slice(4 * step, 4 * step + 4))
+                if c == 0 and step == 1:
+                    hold_gpsimd(first[1][:, 0, CHUNKS - 1, 1, PARTS - 16 : PARTS], F32)
+                    first_level(nc.gpsimd, 1, 1, slice(0, CHUNKS))
                 if c >= 1 and c + 1 < PASSES and step % 2 == 0:
-                    first_level(nc.gpsimd, c + 1, step // 2)
+                    first_level(nc.gpsimd, c + 1, step // 2, slice(0, CHUNKS))
             if i + LEAD < len(units):
                 units[i + LEAD][3]()
             empty()

@@ -38,6 +38,7 @@ T_PER_M = M_TILE // C
 T_PER_N = N_TILE // K
 PAIRS = T // T_PER_M
 LEAD = 2
+VECTOR_ADDS = (1, 3)
 
 FLOPS = 2 * T * C * K * N + 4 * T * N * K
 BYTES = 2 * T * N * C + 2 * T * N * K + 4 * T * C * K
@@ -117,14 +118,16 @@ def tile_iwht3layer_pa_k_kernel(tc, trans, weight, bias, grad_out, out):
 
         def pair_unit(c, step):
             u0, j = step // 2, step % 2
+            vector_adds = step in VECTOR_ADDS
             banks = {}
 
             def fill():
-                banks["both"] = sums.tile([PARTS, 4, PARTS], F32, name="bank")
+                banks["other"] = sums.tile([PARTS, 4, PARTS], F32, name="bank")
                 banks["lone"] = sums.tile([PARTS, 4, PARTS], F32, name="bank")
                 for place in range(4):
-                    turn(nc, banks["both"][:, place, :], first[c][:, u0, 4 * j + place, 0, :], ident[:], True, False)
-                    turn(nc, banks["both"][:, place, :], first[c][:, u0, 4 * j + place, 1, :], ident[:], False, True)
+                    if not vector_adds:
+                        turn(nc, banks["other"][:, place, :], first[c][:, u0, 4 * j + place, 0, :], ident[:], True, False)
+                    turn(nc, banks["other"][:, place, :], first[c][:, u0, 4 * j + place, 1, :], ident[:], vector_adds, True)
                 for place in range(4):
                     turn(nc, banks["lone"][:, place, :], first[c][:, u0, 4 * j + place, 0, :], ident[:], True, True)
 
@@ -132,17 +135,26 @@ def tile_iwht3layer_pa_k_kernel(tc, trans, weight, bias, grad_out, out):
                 if step == 0:
                     rows[c] = stages.tile([PARTS, 2, 2, CHUNKS, PARTS], F32, name="rows")
                 plus = rows[c][:, 0, u0, 4 * j : 4 * j + 4, :]
-                nc.scalar.activation(out=plus, in_=banks["both"][:], func=COPY, scale=1.0 / T)
-                nc.vector.scalar_tensor_tensor(
-                    out=rows[c][:, 1, u0, 4 * j : 4 * j + 4, :],
-                    in0=banks["lone"][:],
-                    scalar=2.0 / T,
-                    in1=plus,
-                    op0=MULT,
-                    op1=SUB,
-                )
+                minus = rows[c][:, 1, u0, 4 * j : 4 * j + 4, :]
+                nc.scalar.activation(out=plus, in_=banks["other"][:], func=COPY, scale=1.0 / T)
+                if vector_adds:
+                    nc.scalar.activation(out=minus, in_=banks["other"][:], func=COPY, scale=-1.0 / T)
+                    signed = rows[c][:, :, u0, 4 * j : 4 * j + 4, :].rearrange("a u f e -> a u (f e)")
+                    nc.vector.scalar_tensor_tensor(
+                        out=signed,
+                        in0=banks["lone"][:].rearrange("a f e -> a (f e)").unsqueeze(1).to_broadcast([PARTS, 2, 4 * PARTS]),
+                        scalar=1.0 / T,
+                        in1=signed,
+                        op0=MULT,
+                        op1=ADD,
+                    )
+                else:
+                    nc.vector.scalar_tensor_tensor(
+                        out=minus, in0=banks["lone"][:], scalar=2.0 / T, in1=plus, op0=MULT, op1=SUB
+                    )
                 regroup(c, 2 * step)
-                regroup(c, 2 * step + 1)
+                if c == 0:
+                    regroup(c, 2 * step + 1)
 
             return fill, empty
 
@@ -179,6 +191,8 @@ def tile_iwht3layer_pa_k_kernel(tc, trans, weight, bias, grad_out, out):
                 totals[u] = total
                 if u > 0:
                     round_total(c, u - 1)
+                if c + 1 < PASSES:
+                    regroup(c + 1, 2 * u + 1)
 
             return fill, empty
 

@@ -38,7 +38,8 @@ T_PER_M = M_TILE // C
 T_PER_N = N_TILE // K
 PAIRS = T // T_PER_M
 LEAD = 2
-VECTOR_ADDS = (1, 3)
+BANKS = 8
+VECTOR_ADDS = (0, 2)
 
 FLOPS = 2 * T * C * K * N + 4 * T * N * K
 BYTES = 2 * T * N * C + 2 * T * N * K + 4 * T * C * K
@@ -81,6 +82,9 @@ def tile_iwht3layer_pa_k_kernel(tc, trans, weight, bias, grad_out, out):
         x_packed, gy_packed, totals = {}, {}, {}
         started = set()
         seen = {}
+        owners = []
+        emptied = set()
+        filled = [0]
 
         def load_g(c):
             g_raw[c] = raw.tile([PARTS, 2, 2, SIDE * LANE], BF16, name="g_raw")
@@ -158,46 +162,55 @@ def tile_iwht3layer_pa_k_kernel(tc, trans, weight, bias, grad_out, out):
 
             return fill, empty
 
-        def column_unit(c, u):
-            t = SIDE * u
+        def column_unit(c, u1):
             banks = {}
 
             def fill():
-                banks["a"] = sums.tile([PARTS, 2, HALVES, PARTS], F32, name="bank")
-                banks["b"] = sums.tile([PARTS, 2, HALVES, PARTS], F32, name="bank")
-                for bank, pairs in ((banks["a"], ((0, 2), (1, 3))), (banks["b"], ((0, 1), (0, 3)))):
-                    for place, (one, two) in enumerate(pairs):
+                banks["even"] = sums.tile([PARTS, 2, HALVES, PARTS], F32, name="bank")
+                banks["odd"] = sums.tile([PARTS, 2, HALVES, PARTS], F32, name="bank")
+                for name, (one, two) in (("even", (0, 2)), ("odd", (1, 3))):
+                    for u0 in range(2):
                         for half in range(HALVES):
-                            turn(nc, bank[:, place, half, :], rows[c][:, u // 2, u % 2, HALVES * one + half, :], weave[:], True, False)
-                            turn(nc, bank[:, place, half, :], rows[c][:, u // 2, u % 2, HALVES * two + half, :], weave[:], False, True)
+                            turn(nc, banks[name][:, u0, half, :], rows[c][:, u1, u0, HALVES * one + half, :], weave[:], True, False)
+                            turn(nc, banks[name][:, u0, half, :], rows[c][:, u1, u0, HALVES * two + half, :], weave[:], False, True)
+                for u0 in range(2):
+                    banks[u0] = sums.tile([PARTS, 2, HALVES, PARTS], F32, name="bank")
+                    for place, (one, two) in enumerate(((0, 1), (0, 3))):
+                        for half in range(HALVES):
+                            turn(nc, banks[u0][:, place, half, :], rows[c][:, u1, u0, HALVES * one + half, :], weave[:], True, False)
+                            turn(nc, banks[u0][:, place, half, :], rows[c][:, u1, u0, HALVES * two + half, :], weave[:], False, True)
 
             def empty():
-                if u == 0:
+                if u1 == 0:
                     gy_grouped[c] = grouped.tile([PARTS, T, LANE], BF16, name="gy_grouped", align_bytes=64)
-                odd = small.tile([PARTS, LANE], F32, name="odd")
-                total = small.tile([PARTS, LANE], F32, name="total")
-                even = banks["a"][:, 0, :, :].rearrange("a h e -> a (h e)")
-                nc.scalar.copy(out=odd[:], in_=banks["a"][:, 1, :, :].rearrange("a h e -> a (h e)"))
+                by_v = gy_grouped[c][:].rearrange("a (u v) e -> a u v e", v=SIDE)[:, 2 * u1 : 2 * u1 + 2]
+                odd = small.tile([PARTS, 2, LANE], F32, name="odd")
+                total = small.tile([PARTS, 2, LANE], F32, name="total")
+                even = banks["even"][:].rearrange("a u h e -> a u (h e)")
+                nc.scalar.copy(out=odd[:], in_=banks["odd"][:].rearrange("a u h e -> a u (h e)"))
                 nc.vector.tensor_tensor(out=total[:], in0=even, in1=odd[:], op=ADD)
-                nc.vector.tensor_tensor(out=gy_grouped[c][:, t + 1, :], in0=even, in1=odd[:], op=SUB)
-                nc.vector.scalar_tensor_tensor(
-                    out=gy_grouped[c][:, t + 2 : t + 4, :],
-                    in0=banks["b"][:].rearrange("a v h e -> a v (h e)"),
-                    scalar=2.0,
-                    in1=total[:].unsqueeze(1).to_broadcast([PARTS, 2, LANE]),
-                    op0=MULT,
-                    op1=SUB,
-                )
-                totals[u] = total
-                if u > 0:
-                    round_total(c, u - 1)
+                nc.vector.tensor_tensor(out=by_v[:, :, 1, :], in0=even, in1=odd[:], op=SUB)
+                for u0 in range(2):
+                    nc.vector.scalar_tensor_tensor(
+                        out=by_v[:, u0, 2:4, :],
+                        in0=banks[u0][:].rearrange("a v h e -> a v (h e)"),
+                        scalar=2.0,
+                        in1=total[:, u0, :].unsqueeze(1).to_broadcast([PARTS, 2, LANE]),
+                        op0=MULT,
+                        op1=SUB,
+                    )
+                totals[u1] = total
+                if u1 > 0:
+                    round_total(c, u1 - 1)
                 if c + 1 < PASSES:
-                    regroup(c + 1, 2 * u + 1)
+                    regroup(c + 1, 4 * u1 + 1)
+                    regroup(c + 1, 4 * u1 + 3)
 
             return fill, empty
 
-        def round_total(c, u):
-            nc.scalar.copy(out=gy_grouped[c][:, SIDE * u, :], in_=totals[u][:])
+        def round_total(c, u1):
+            by_v = gy_grouped[c][:].rearrange("a (u v) e -> a u v e", v=SIDE)[:, 2 * u1 : 2 * u1 + 2]
+            nc.scalar.copy(out=by_v[:, :, 0, :], in_=totals[u1][:])
 
         def quantise_x(c):
             codes = packed.tile([PARTS, COLS], U32, name="x_codes", align_bytes=64)
@@ -248,13 +261,15 @@ def tile_iwht3layer_pa_k_kernel(tc, trans, weight, bias, grad_out, out):
                 started.add(s)
 
         def window(c):
-            round_total(c, SIDE - 1)
+            round_total(c, 1)
             last = c == PASSES - 1
             made = []
             for s in range(PAIRS) if last else (2 * (c % 4), 2 * (c % 4) + 1):
                 passes = list(range(seen.get(s, 0), c))
                 if passes or last:
+                    assert room(1)
                     bank = sums.tile([M_TILE, N_TILE], F32, name="bank")
+                    owners.append(("product", c, s))
                     for done in passes:
                         mx_pass(bank, s, done, done == passes[0], done == passes[-1] and not last)
                     made.append((s, bank, not passes))
@@ -268,14 +283,28 @@ def tile_iwht3layer_pa_k_kernel(tc, trans, weight, bias, grad_out, out):
                     mx_pass(bank, s, c, fresh, True)
             for s, bank, fresh in made:
                 collect(s, bank)
+                emptied.add(("product", c, s))
 
         units = []
         for c in range(-1, PASSES):
             for step in range(STEPS):
                 if c + 1 < PASSES:
-                    units.append(("pair", c + 1, step) + pair_unit(c + 1, step))
-                if c >= 0:
-                    units.append(("column", c, step) + column_unit(c, step))
+                    units.append(("pair", c + 1, step, 2) + pair_unit(c + 1, step))
+                if c >= 0 and step % 2 == 1:
+                    units.append(("column", c, step // 2, 4) + column_unit(c, step // 2))
+
+        def room(need):
+            handed = len(owners)
+            return all(handed + i < BANKS or owners[handed + i - BANKS] in emptied for i in range(need))
+
+        def fill_ahead(upto):
+            while filled[0] <= min(upto, len(units) - 1):
+                need = units[filled[0]][3]
+                if not room(need):
+                    return
+                owners.extend([filled[0]] * need)
+                units[filled[0]][4]()
+                filled[0] += 1
 
         load_g(0)
         load_x(0)
@@ -286,9 +315,7 @@ def tile_iwht3layer_pa_k_kernel(tc, trans, weight, bias, grad_out, out):
         for u0 in range(2):
             for j in range(2):
                 first_level(nc.vector, 0, u0, slice(4 * j, 4 * j + 4))
-        for ahead in range(LEAD):
-            units[ahead][3]()
-        for i, (kind, c, step, fill, empty) in enumerate(units):
+        for i, (kind, c, step, need, fill, empty) in enumerate(units):
             if kind == "pair":
                 if step == 0 and c + 2 < PASSES:
                     load_g(c + 2)
@@ -301,10 +328,10 @@ def tile_iwht3layer_pa_k_kernel(tc, trans, weight, bias, grad_out, out):
                     first_level(nc.gpsimd, 1, 1, slice(0, CHUNKS))
                 if c >= 1 and c + 1 < PASSES and step % 2 == 0:
                     first_level(nc.gpsimd, c + 1, step // 2, slice(0, CHUNKS))
-            if i + LEAD < len(units):
-                units[i + LEAD][3]()
+            fill_ahead(i + LEAD)
             empty()
-            if kind == "column" and step == STEPS - 1:
+            emptied.add(i)
+            if kind == "column" and step == 1:
                 window(c)
 
         out_view = out.rearrange("(s two) c k -> two c s k", two=T_PER_M)

from contextlib import ExitStack

import concourse.mybir as mybir
from concourse.masks import make_identity

F32 = mybir.dt.float32
BF16 = mybir.dt.bfloat16
U32 = mybir.dt.uint32
U8 = mybir.dt.uint8
E4M3_X4 = mybir.dt.float8_e4m3fn_x4
E5M2_X4 = mybir.dt.float8_e5m2_x4
ADD = mybir.AluOpType.add
SUB = mybir.AluOpType.subtract
MULT = mybir.AluOpType.mult
COPY = mybir.ActivationFunctionType.Copy

PARTS = 128
PACK = 4
K_PASS = PARTS * PACK

B, NH, NW, C, K, SIDE = 8, 32, 32, 64, 64, 4
T = SIDE * SIDE
N = B * NH * NW
PASSES = N // K_PASS
ROWS_PER_PASS = K_PASS // NW
PARTS_PER_ROW = NW // PACK
COLS = T * K
LANE = K * PACK
HALVES = LANE // PARTS
K_HALF = K // HALVES
CHUNKS = SIDE * HALVES
STEPS = 4
PIECES = 8

M_TILE = 128
N_TILE = 512
T_PER_M = M_TILE // C
T_PER_N = N_TILE // K
PAIRS = T // T_PER_M
LEAD = 2
BANKS = 8
VECTOR_ADDS = (0, 2)

FLOPS = 2 * T * C * K * N + 4 * T * N * K
BYTES = 2 * T * N * C + 2 * T * N * K + 4 * T * C * K


def turn(nc, out, tile, moving, start, stop):
    nc.tensor.matmul(out=out, lhsT=tile, rhs=moving, is_transpose=True, start=start, stop=stop)


def tile_iwht3layer_pa_k_kernel(tc, trans, weight, bias, grad_out, out):
    nc = tc.nc

    x_dram = trans.rearrange(
        "t b (h i) (r tau) c -> (b h) (i r) t (tau c)", h=2, i=ROWS_PER_PASS, r=PARTS_PER_ROW, tau=PACK
    )
    g_dram = grad_out.rearrange(
        "b (h i p) (r e) k -> (b h) p i r (e k)", h=2, i=ROWS_PER_PASS, p=SIDE, r=PARTS_PER_ROW, e=PACK * SIDE
    )

    with ExitStack() as ctx:
        ctx.enter_context(tc.manual_schedule())
        const = ctx.enter_context(tc.tile_pool(name="const", bufs=1))
        raw = ctx.enter_context(tc.tile_pool(name="raw", bufs=3))
        stages = ctx.enter_context(tc.tile_pool(name="stages", bufs=2))
        small = ctx.enter_context(tc.tile_pool(name="small", bufs=4))
        grouped = ctx.enter_context(tc.tile_pool(name="grouped", bufs=3))
        packed = ctx.enter_context(tc.tile_pool(name="packed", bufs=5))
        sums = ctx.enter_context(tc.psum_pool(name="sums", bufs=8))

        ident = const.tile([PARTS, PARTS], F32)
        make_identity(nc, ident[:])
        weave = const.tile([PARTS, PARTS], F32)
        nc.vector.tensor_copy(
            out=weave[:].rearrange("a (kk tau) -> a kk tau", tau=PACK),
            in_=ident[:].rearrange("a (tau kk) -> a kk tau", tau=PACK),
        )
        result = const.tile([M_TILE, PAIRS, M_TILE], F32)

        g_raw, x_raw, first, rows, x_grouped, gy_grouped = {}, {}, {}, {}, {}, {}
        x_packed, gy_packed, totals = {}, {}, {}
        started = set()
        seen = {}
        owners = []
        emptied = set()
        filled = [0]

        def load_g(c):
            g_raw[c] = raw.tile([PARTS, 2, 2, SIDE * LANE], BF16, name="g_raw")
            for p in range(SIDE):
                nc.sync.dma_start(out=g_raw[c][:, p % 2, p // 2, :], in_=g_dram[c, p])

        def load_x(c):
            x_raw[c] = raw.tile([PARTS, T, LANE], BF16, name="x_raw")
            nc.sync.dma_start(out=x_raw[c][:], in_=x_dram[c])

        def first_level(engine, c, u0, chunks):
            if u0 == 0 and chunks.start == 0:
                first[c] = stages.tile([PARTS, 2, CHUNKS, 2, PARTS], F32, name="first")
            upper, lower = [
                g_raw[c][:, p0, :, :].rearrange("a p1 e -> a (p1 e)").rearrange("a (pt qh kk) -> a qh pt kk", pt=2 * PACK, qh=CHUNKS)[
                    :, chunks
                ]
                for p0 in range(2)
            ]
            engine.tensor_tensor(
                out=first[c][:, u0, chunks, :, :].rearrange("a qh p1 e -> a (qh p1 e)").rearrange("a (qh pt kk) -> a qh pt kk", pt=2 * PACK, kk=K_HALF),
                in0=upper,
                in1=lower,
                op=ADD if u0 == 0 else SUB,
            )

        def regroup(c, piece):
            if piece == 0:
                x_grouped[c] = grouped.tile([PARTS, T, LANE], BF16, name="x_grouped", align_bytes=64)
            first_t = 2 * piece
            nc.scalar.copy(
                out=x_grouped[c][:, first_t : first_t + 2, :].rearrange("a t (c tau) -> a t c tau", tau=PACK),
                in_=x_raw[c][:, first_t : first_t + 2, :].rearrange("a t (tau c) -> a t c tau", tau=PACK),
            )

        def pair_unit(c, step):
            u0, j = step // 2, step % 2
            vector_adds = step in VECTOR_ADDS
            banks = {}

            def fill():
                banks["other"] = sums.tile([PARTS, 4, PARTS], F32, name="bank")
                banks["lone"] = sums.tile([PARTS, 4, PARTS], F32, name="bank")
                for place in range(4):
                    if not vector_adds:
                        turn(nc, banks["other"][:, place, :], first[c][:, u0, 4 * j + place, 0, :], ident[:], True, False)
                    turn(nc, banks["other"][:, place, :], first[c][:, u0, 4 * j + place, 1, :], ident[:], vector_adds, True)
                for place in range(4):
                    turn(nc, banks["lone"][:, place, :], first[c][:, u0, 4 * j + place, 0, :], ident[:], True, True)

            def empty():
                if step == 0:
                    rows[c] = stages.tile([PARTS, 2, 2, CHUNKS, PARTS], F32, name="rows")
                plus = rows[c][:, 0, u0, 4 * j : 4 * j + 4, :]
                minus = rows[c][:, 1, u0, 4 * j : 4 * j + 4, :]
                nc.scalar.activation(out=plus, in_=banks["other"][:], func=COPY, scale=1.0 / T)
                if vector_adds:
                    nc.scalar.activation(out=minus, in_=banks["other"][:], func=COPY, scale=-1.0 / T)
                    signed = rows[c][:, :, u0, 4 * j : 4 * j + 4, :].rearrange("a u f e -> a u (f e)")
                    nc.vector.scalar_tensor_tensor(
                        out=signed,
                        in0=banks["lone"][:].rearrange("a f e -> a (f e)").unsqueeze(1).to_broadcast([PARTS, 2, 4 * PARTS]),
                        scalar=1.0 / T,
                        in1=signed,
                        op0=MULT,
                        op1=ADD,
                    )
                else:
                    nc.vector.scalar_tensor_tensor(
                        out=minus, in0=banks["lone"][:], scalar=2.0 / T, in1=plus, op0=MULT, op1=SUB
                    )
                regroup(c, 2 * step)
                if c == 0:
                    regroup(c, 2 * step + 1)

            return fill, empty

        def column_unit(c, u1):
            banks = {}

            def fill():
                banks["even"] = sums.tile([PARTS, 2, HALVES, PARTS], F32, name="bank")
                banks["odd"] = sums.tile([PARTS, 2, HALVES, PARTS], F32, name="bank")
                for name, (one, two) in (("even", (0, 2)), ("odd", (1, 3))):
                    for u0 in range(2):
                        for half in range(HALVES):
                            turn(nc, banks[name][:, u0, half, :], rows[c][:, u1, u0, HALVES * one + half, :], weave[:], True, False)
                            turn(nc, banks[name][:, u0, half, :], rows[c][:, u1, u0, HALVES * two + half, :], weave[:], False, True)
                for u0 in range(2):
                    banks[u0] = sums.tile([PARTS, 2, HALVES, PARTS], F32, name="bank")
                    for place, (one, two) in enumerate(((0, 1), (0, 3))):
                        for half in range(HALVES):
                            turn(nc, banks[u0][:, place, half, :], rows[c][:, u1, u0, HALVES * one + half, :], weave[:], True, False)
                            turn(nc, banks[u0][:, place, half, :], rows[c][:, u1, u0, HALVES * two + half, :], weave[:], False, True)

            def empty():
                if u1 == 0:
                    gy_grouped[c] = grouped.tile([PARTS, T, LANE], BF16, name="gy_grouped", align_bytes=64)
                by_v = gy_grouped[c][:].rearrange("a (u v) e -> a u v e", v=SIDE)[:, 2 * u1 : 2 * u1 + 2]
                odd = small.tile([PARTS, 2, LANE], F32, name="odd")
                total = small.tile([PARTS, 2, LANE], F32, name="total")
                even = banks["even"][:].rearrange("a u h e -> a u (h e)")
                nc.scalar.copy(out=odd[:], in_=banks["odd"][:].rearrange("a u h e -> a u (h e)"))
                nc.vector.tensor_tensor(out=total[:], in0=even, in1=odd[:], op=ADD)
                nc.vector.tensor_tensor(out=by_v[:, :, 1, :], in0=even, in1=odd[:], op=SUB)
                for u0 in range(2):
                    nc.vector.scalar_tensor_tensor(
                        out=by_v[:, u0, 2:4, :],
                        in0=banks[u0][:].rearrange("a v h e -> a v (h e)"),
                        scalar=2.0,
                        in1=total[:, u0, :].unsqueeze(1).to_broadcast([PARTS, 2, LANE]),
                        op0=MULT,
                        op1=SUB,
                    )
                totals[u1] = total
                if u1 > 0:
                    round_total(c, u1 - 1)
                if c + 1 < PASSES:
                    regroup(c + 1, 4 * u1 + 1)
                    regroup(c + 1, 4 * u1 + 3)

            return fill, empty

        def round_total(c, u1):
            by_v = gy_grouped[c][:].rearrange("a (u v) e -> a u v e", v=SIDE)[:, 2 * u1 : 2 * u1 + 2]
            nc.scalar.copy(out=by_v[:, :, 0, :], in_=totals[u1][:])

        def quantise_x(c):
            codes = packed.tile([PARTS, COLS], U32, name="x_codes", align_bytes=64)
            scales = packed.tile([PARTS, COLS], U8, name="x_scales", align_bytes=64)
            nc.vector.quantize_mx(
                out=codes[:].bitcast(E4M3_X4), scales=scales[:], in_=x_grouped[c][:].rearrange("a t e -> a (t e)")
            )
            x_packed[c] = (codes, scales)

        def quantise_gy(c, parts):
            if c not in gy_packed:
                codes = packed.tile([PARTS, COLS], U32, name="gy_codes", align_bytes=64)
                scales = packed.tile([PARTS, COLS], U8, name="gy_scales", align_bytes=64)
                gy_packed[c] = (codes, scales)
            codes, scales = gy_packed[c]
            cols = slice(parts[0] * COLS // 2, (parts[-1] + 1) * COLS // 2)
            nc.vector.quantize_mx(
                out=codes[:, cols].bitcast(E5M2_X4),
                scales=scales[:, cols],
                in_=gy_grouped[c][:, parts[0] * T // 2 : (parts[-1] + 1) * T // 2, :].rearrange("a t e -> a (t e)"),
            )

        def hold_gpsimd(written, dtype):
            junk = small.tile([PARTS, 16], dtype, name="junk")
            nc.gpsimd.tensor_copy(out=junk[:], in_=written)

        def mx_pass(bank, s, c, start, stop):
            m_cols = slice(s * M_TILE, (s + 1) * M_TILE)
            n_first = (s * T_PER_M // T_PER_N) * N_TILE
            n_cols = slice(n_first, n_first + N_TILE)
            nc.tensor.matmul_mx(
                out=bank[:],
                lhsT=x_packed[c][0][:, m_cols].bitcast(E4M3_X4),
                lhsT_scale=x_packed[c][1][:, m_cols],
                rhs=gy_packed[c][0][:, n_cols].bitcast(E5M2_X4),
                rhs_scale=gy_packed[c][1][:, n_cols],
                start=start,
                stop=stop,
            )

        def collect(s, bank):
            n_first = (s * T_PER_M // T_PER_N) * N_TILE
            wanted = slice(s * M_TILE - n_first, (s + 1) * M_TILE - n_first)
            if s in started:
                nc.vector.tensor_tensor(out=result[:, s, :], in0=bank[:, wanted], in1=result[:, s, :], op=ADD)
            else:
                nc.vector.tensor_copy(out=result[:, s, :], in_=bank[:, wanted])
                started.add(s)

        def window(c):
            round_total(c, 1)
            last = c == PASSES - 1
            made = []
            for s in range(PAIRS) if last else (2 * (c % 4), 2 * (c % 4) + 1):
                passes = list(range(seen.get(s, 0), c))
                if passes or last:
                    assert room(1)
                    bank = sums.tile([M_TILE, N_TILE], F32, name="bank")
                    owners.append(("product", c, s))
                    for done in passes:
                        mx_pass(bank, s, done, done == passes[0], done == passes[-1] and not last)
                    made.append((s, bank, not passes))
                    seen[s] = c
            quantise_x(c)
            quantise_gy(c, (0, 1))
            if c + 3 < PASSES:
                hold_gpsimd(gy_packed[c][0][:, 0:16], U32)
            for s, bank, fresh in made:
                if last:
                    mx_pass(bank, s, c, fresh, True)
            for s, bank, fresh in made:
                collect(s, bank)
                emptied.add(("product", c, s))

        units = []
        for c in range(-1, PASSES):
            for step in range(STEPS):
                if c + 1 < PASSES:
                    units.append(("pair", c + 1, step, 2) + pair_unit(c + 1, step))
                if c >= 0 and step % 2 == 1:
                    units.append(("column", c, step // 2, 4) + column_unit(c, step // 2))

        def room(need):
            handed = len(owners)
            return all(handed + i < BANKS or owners[handed + i - BANKS] in emptied for i in range(need))

        def fill_ahead(upto):
            while filled[0] <= min(upto, len(units) - 1):
                need = units[filled[0]][3]
                if not room(need):
                    return
                owners.extend([filled[0]] * need)
                units[filled[0]][4]()
                filled[0] += 1

        load_g(0)
        load_x(0)
        load_g(1)
        warm = const.tile([PARTS, 1], F32)
        nc.vector.memset(warm[:], 0.0)
        nc.scalar.activation(out=warm[:], in_=warm[:], func=COPY, scale=1.0)
        for u0 in range(2):
            for j in range(2):
                first_level(nc.vector, 0, u0, slice(4 * j, 4 * j + 4))
        for i, (kind, c, step, need, fill, empty) in enumerate(units):
            if kind == "pair":
                if step == 0 and c + 2 < PASSES:
                    load_g(c + 2)
                if step == 0 and c + 1 < PASSES:
                    load_x(c + 1)
                if c == 0 and step < 2:
                    first_level(nc.vector, 1, 0, slice(4 * step, 4 * step + 4))
                if c == 0 and step == 1:
                    hold_gpsimd(first[1][:, 0, CHUNKS - 1, 1, PARTS - 16 : PARTS], F32)
                    first_level(nc.gpsimd, 1, 1, slice(0, CHUNKS))
                if c >= 1 and c + 1 < PASSES and step % 2 == 0:
                    first_level(nc.gpsimd, c + 1, step // 2, slice(0, CHUNKS))
            fill_ahead(i + LEAD)
            empty()
            emptied.add(i)
            if kind == "column" and step == 1:
                window(c)

        out_view = out.rearrange("(s two) c k -> two c s k", two=T_PER_M)
        nc.sync.dma_start(out=out_view[0], in_=result[0:C, :, 0:K])
        nc.scalar.dma_start(out=out_view[1], in_=result[C:M_TILE, :, K:M_TILE])
